import numpy as np
import ml_dtypes


def mxq(x, axis, fmt="e4m3"):
    dtype, down = {"e4m3": (ml_dtypes.float8_e4m3fn, 7), "e5m2": (ml_dtypes.float8_e5m2, 14)}[fmt]
    v = np.moveaxis(np.asarray(x, np.float32).astype(ml_dtypes.bfloat16).astype(np.float64), axis, -1)
    blocks = v.reshape(v.shape[:-1] + (-1, 32))
    amax = np.abs(blocks).max(-1, keepdims=True)
    byte = np.maximum(np.where(amax > 0, np.frexp(amax)[1] - 1 + 127, 0) - down, 1)
    scale = np.exp2(byte - 127.0)
    codes = (blocks / scale).astype(np.float32).astype(dtype).astype(np.float64)
    return np.moveaxis((codes * scale).reshape(v.shape), -1, axis)


WIDE = False


def mx_kscale(k):
    if not WIDE:
        return np.ones(k)
    levels = np.array([10, -10, 5, -5, 0])
    a = np.random.permutation(np.resize(levels, k // 512 * 4)).reshape(k // 512, 4)
    idx = np.arange(k)
    return np.exp2(a[idx // 512, idx % 128 // 32])


BF16 = ml_dtypes.bfloat16


def bf(x):
    return np.asarray(x, np.float32).astype(BF16)


def f64(x):
    return np.asarray(x).astype(np.float64)


BS, P, C, D, E = 512, 1152, 8, 16, 8
K = P * E
N = C * D


def setup_inputs():
    s = mx_kscale(K).reshape(P, E)
    x = np.random.standard_normal((BS, P, E)) * s
    W = np.random.standard_normal((1, P, C, D, E)) * np.sqrt(P / E) / s[None, :, None, None, :]
    return {"x": bf(x), "W": bf(W)}


def reference(x, W):
    xf = f64(x).reshape(BS, K)
    wf = f64(W)[0].transpose(0, 3, 1, 2).reshape(K, N)
    tot = (mxq(xf, 1, "e4m3") @ mxq(wf, 0, "e4m3")).reshape(BS, 1, C, D)
    s = tot / P
    s = s[..., None]
    norm2 = s * s
    v = norm2 / (1.0 + norm2) * (s / np.sqrt(norm2))
    return np.squeeze(v, axis=1)

@@ -1,0 +1,233 @@
+from contextlib import ExitStack
+
+import concourse.mybir as mybir
+from concourse.masks import make_identity
+
+F32 = mybir.dt.float32
+BF16 = mybir.dt.bfloat16
+U32 = mybir.dt.uint32
+U8 = mybir.dt.uint8
+FP8X4 = mybir.dt.float8_e4m3fn_x4
+ACTF = mybir.ActivationFunctionType
+ALU = mybir.AluOpType
+
+P = 128
+BS = 512
+K = 9216
+N = 128
+PASSES = K // 512
+FLOPS = 2 * BS * K * N
+
+W_CHUNKS = [(0, 1), (1, 3), (3, 6), (6, 9)]
+X_CHUNKS = [(0, 6), (6, 12), (12, 18)]
+X_CHUNKS_LAST = [(0, 6), (6, 12), (12, 16), (16, 18)]
+GROUPS = [[2, 2], [2, 2], [2, 2], [2, 2], [2]]
+GROUPS_LAST = [[2, 2], [2, 2], [2, 2], [2], [2], [1, 1]]
+BANKS = 6
+MX_LAG = 5
+
+
+def tile_digitcaps_kernel(tc, x, W, out):
+    nc = tc.nc
+    x_rows = x.rearrange("b p e -> b (p e)")
+    w_rows = W.rearrange("o (g q) c d e -> q (o g) (c d e)", q=P)
+    out_rows = out.rearrange("b c d o -> b (c d o)")
+
+    with ExitStack() as ctx:
+        keep = ctx.enter_context(tc.tile_pool(name="keep", bufs=1))
+        stage = ctx.enter_context(tc.tile_pool(name="stage", bufs=4))
+        small = ctx.enter_context(tc.tile_pool(name="small", bufs=2))
+        psum = ctx.enter_context(tc.psum_pool(name="psum", bufs=1))
+        ctx.enter_context(tc.manual_schedule())
+
+        w_words = {}
+        for k, (g0, g1) in enumerate(W_CHUNKS):
+            wp = keep.tile([P, (g1 - g0) * 1024], BF16, name="wp%d" % k)
+            nc.sync.dma_start(
+                out=wp[:].rearrange("q (g f) -> q g f", f=1024), in_=w_rows[:, g0:g1, :]
+            )
+            words = wp[:].bitcast(F32)
+            for g in range(g0, g1):
+                w_words[g] = words[:, (g - g0) * 512 : (g - g0 + 1) * 512].rearrange(
+                    "q (n e) -> q n e", e=4
+                )
+        src_words = {}
+        for r in range(1, 5):
+            chunks = X_CHUNKS_LAST if r == 4 else X_CHUNKS
+            for k, (p0, p1) in enumerate(chunks):
+                xt = keep.tile([P, (p1 - p0) * 512], BF16, name="x%d_%d" % (r, k))
+                nc.sync.dma_start(
+                    out=xt[:], in_=x_rows[(r - 1) * P : r * P, p0 * 512 : p1 * 512]
+                )
+                words = xt[:].bitcast(F32)
+                for g in range(p0, p1):
+                    src_words[(r, g)] = (words, (g - p0) * 256)
+
+        ident = keep.tile([P, P], F32, name="ident")
+        make_identity(nc, ident[:])
+        warm = keep.tile([P, 2], F32, name="warm")
+        nc.vector.memset(warm[:], 0.0)
+        nc.scalar.activation(out=warm[:, 1:2], in_=warm[:, 0:1], func=ACTF.Square)
+
+        codes = {}
+        planes = {}
+        for r in range(5):
+            codes[r] = keep.tile([P, PASSES * P], U32, name="codes%d" % r, align_bytes=64)
+            planes[r] = keep.tile([P, PASSES * P], U8, name="planes%d" % r, align_bytes=64)
+
+        groups = {}
+        row_units = {}
+        for r in range(5):
+            plan = GROUPS_LAST if r == 4 else GROUPS
+            row_units[r] = []
+            p0 = 0
+            for gi, sizes in enumerate(plan):
+                groups[(r, gi)] = [p0, sum(sizes), 0, 1]
+                off = 0
+                for np_ in sizes:
+                    row_units[r].append(("B", r, p0 + off, np_, (r, gi), off))
+                    off += np_
+                p0 += off
+        order = [("A", 0), ("A", 1), ("A", 2)]
+        for w in range(9):
+            order.append(row_units[0][w])
+            if w + 3 < 9:
+                order.append(("A", w + 3))
+        for r in range(1, 5):
+            order.extend(row_units[r])
+        n_units = len(order)
+        last_index = {}
+        for i, unit in enumerate(order):
+            if unit[0] == "B":
+                groups[unit[4]][2] = i
+                last_index[unit[1]] = i
+        groups[(4, len(GROUPS_LAST) - 1)][3] = 0
+
+        q_at = {}
+        for key in sorted(groups):
+            g = groups[key]
+            step = g[2] + 1 + g[3]
+            q_at[step] = q_at.get(step, []) + [key]
+        mx_pre = {}
+        mx_post = {}
+        sq_a = {}
+        sq_b = {}
+        sq_c = {}
+        for r in range(1, 4):
+            s = last_index[r] + MX_LAG
+            mx_pre[s] = (r, 0, PASSES)
+            sq_a[s + 2] = r
+            sq_b[s + 3] = r
+            sq_c[s + 4] = r
+        mx_pre[n_units] = (4, 0, PASSES - 2)
+        mx_post[n_units] = (4, PASSES - 2, PASSES)
+        sq_a[n_units] = 4
+        sq_b[n_units] = 4
+        sq_c[n_units] = 4
+
+        def on_vector(unit, i):
+            if unit[0] == "A":
+                return unit[1] % 2 == 1
+            r, p0 = unit[1], unit[2]
+            if r == 0:
+                return p0 in (2, 8, 14)
+            if r == 4 and p0 == PASSES - 1:
+                return True
+            return p0 == 8
+
+        banks = {}
+        s_tiles = {}
+        grouped = {}
+        acc = {}
+        sq = {}
+        c_inv = 1.0 / 1152.0
+
+        def run_mx(r, g0, g1):
+            if g0 == 0:
+                acc[r] = psum.tile([P, N], F32, name="acc%d" % (r % 2), tag="acc%d" % (r % 2))
+            for g in range(g0, g1):
+                cols = slice(g * P, (g + 1) * P)
+                nc.tensor.matmul_mx(
+                    out=acc[r][:],
+                    lhsT=codes[r][:, cols].bitcast(FP8X4),
+                    lhsT_scale=planes[r][:, cols],
+                    rhs=codes[0][:, cols].bitcast(FP8X4),
+                    rhs_scale=planes[0][:, cols],
+                    start=(g == 0),
+                    stop=(g == PASSES - 1),
+                )
+
+        for step in range(n_units + 1):
+            if step < n_units:
+                unit = order[step]
+                ps = psum.tile([P, 512], F32, name="tp%d" % (step % BANKS), tag="tp%d" % (step % BANKS))
+                banks[step] = ps
+                if unit[0] == "A":
+                    for e in range(4):
+                        nc.tensor.transpose(
+                            out=ps[:, e * P : (e + 1) * P], in_=w_words[unit[1]][:, :, e], identity=ident[:]
+                        )
+                else:
+                    r, p0, np_ = unit[1], unit[2], unit[3]
+                    for i in range(2 * np_):
+                        if r == 0:
+                            src = s_tiles[p0 // 2][:, i * P : (i + 1) * P]
+                        else:
+                            words, off = src_words[(r, p0 + i // 2)]
+                            src = words[:, off + (i % 2) * P : off + (i % 2 + 1) * P]
+                        nc.tensor.transpose(out=ps[:, i * P : (i + 1) * P], in_=src, identity=ident[:])
+            if step in mx_pre:
+                run_mx(*mx_pre[step])
+            if step >= 1:
+                unit = order[step - 1]
+                ps = banks[step - 1]
+                if unit[0] == "A":
+                    st = keep.tile([P, 512], F32, name="s%d" % unit[1])
+                    s_tiles[unit[1]] = st
+                    dst = st[:].rearrange("n (p e) -> n p e", e=4)
+                    src = ps[:].rearrange("n (e p) -> n p e", e=4)
+                else:
+                    np_, key, off = unit[3], unit[4], unit[5]
+                    if off == 0:
+                        grouped[key] = stage.tile([P, groups[key][1] * 512], BF16, name="grp", tag="grp", align_bytes=64)
+                    dst = grouped[key][:].bitcast(F32)[:, off * 256 : (off + np_) * 256].rearrange(
+                        "q (c b u) -> q c b u", c=np_, u=2
+                    )
+                    src = ps[:, 0 : np_ * 256].rearrange("q (c u b) -> q c b u", c=np_, u=2)
+                if on_vector(unit, step - 1):
+                    nc.vector.tensor_copy(out=dst, in_=src)
+                else:
+                    nc.scalar.copy(out=dst, in_=src)
+            for key in q_at.get(step, []):
+                p0, np_ = groups[key][0], groups[key][1]
+                cols = slice(p0 * P, (p0 + np_) * P)
+                nc.vector.quantize_mx(
+                    out=codes[key[0]][:, cols].bitcast(FP8X4),
+                    scales=planes[key[0]][:, cols],
+                    in_=grouped[key][:],
+                )
+            if step in mx_post:
+                run_mx(*mx_post[step])
+            if step in sq_a:
+                r = sq_a[step]
+                q = small.tile([P, N], F32, name="q")
+                a = small.tile([P, N], F32, name="a")
+                nc.scalar.activation(out=q[:], in_=acc[r][:], func=ACTF.Square, scale=c_inv)
+                nc.scalar.activation(out=a[:], in_=acc[r][:], func=ACTF.Abs, scale=c_inv)
+                sq[r] = [q, a]
+            if step in sq_b:
+                r = sq_b[step]
+                den = small.tile([P, N], F32, name="den")
+                rec = small.tile([P, N], F32, name="rec")
+                nc.vector.tensor_scalar_add(out=den[:], in0=sq[r][0][:], scalar1=1.0)
+                nc.vector.reciprocal(out=rec[:], in_=den[:])
+                sq[r].append(rec)
+            if step in sq_c:
+                r = sq_c[step]
+                t = small.tile([P, N], F32, name="t")
+                v = small.tile([P, N], F32, name="v")
+                nc.vector.scalar_tensor_tensor(
+                    out=t[:], in0=acc[r][:], scalar=c_inv, in1=sq[r][2][:], op0=ALU.mult, op1=ALU.mult
+                )
+                nc.vector.tensor_tensor(out=v[:], in0=t[:], in1=sq[r][1][:], op=ALU.mult)
+                nc.sync.dma_start(out=out_rows[(r - 1) * P : r * P, :], in_=v[:])

@@ -16,15 +16,15 @@ BS = 512
 K = 9216
 N = 128
 PASSES = K // 512
+B_TILES = BS // P
 FLOPS = 2 * BS * K * N
 
-W_CHUNKS = [(0, 1), (1, 3), (3, 6), (6, 9)]
+W_CHUNKS = [(0, 1), (1, 2), (2, 3), (3, 4), (4, 5), (5, 6), (6, 7), (7, 8), (8, 9)]
 X_CHUNKS = [(0, 6), (6, 12), (12, 18)]
 X_CHUNKS_LAST = [(0, 6), (6, 12), (12, 16), (16, 18)]
-GROUPS = [[2, 2], [2, 2], [2, 2], [2, 2], [2]]
-GROUPS_LAST = [[2, 2], [2, 2], [2, 2], [2], [2], [1, 1]]
 BANKS = 6
-MX_LAG = 5
+PERIOD = 4
+IDLE_AFTER = {8: 4, 12: 1, 16: 1, 21: 1}
 
 
 def tile_digitcaps_kernel(tc, x, W, out):
@@ -51,89 +51,89 @@ def tile_digitcaps_kernel(tc, x, W, out):
                 w_words[g] = words[:, (g - g0) * 512 : (g - g0 + 1) * 512].rearrange(
                     "q (n e) -> q n e", e=4
                 )
-        src_words = {}
-        for r in range(1, 5):
-            chunks = X_CHUNKS_LAST if r == 4 else X_CHUNKS
+        x_words = {}
+        for r in range(B_TILES):
+            chunks = X_CHUNKS_LAST if r == B_TILES - 1 else X_CHUNKS
             for k, (p0, p1) in enumerate(chunks):
                 xt = keep.tile([P, (p1 - p0) * 512], BF16, name="x%d_%d" % (r, k))
-                nc.sync.dma_start(
-                    out=xt[:], in_=x_rows[(r - 1) * P : r * P, p0 * 512 : p1 * 512]
-                )
+                nc.sync.dma_start(out=xt[:], in_=x_rows[r * P : (r + 1) * P, p0 * 512 : p1 * 512])
                 words = xt[:].bitcast(F32)
                 for g in range(p0, p1):
-                    src_words[(r, g)] = (words, (g - p0) * 256)
+                    x_words[r * PASSES + g] = (words, (g - p0) * 256)
 
+        zeros = keep.tile([P, P], F32, name="zeros")
+        warm = keep.tile([P, 2], F32, name="warm")
+        nc.vector.memset(zeros[:], 0.0)
+        nc.vector.memset(warm[:], 1.0)
+        nc.scalar.activation(out=warm[:, 1:2], in_=warm[:, 0:1], func=ACTF.Abs_reciprocal_sqrt)
         ident = keep.tile([P, P], F32, name="ident")
         make_identity(nc, ident[:])
-        warm = keep.tile([P, 2], F32, name="warm")
-        nc.vector.memset(warm[:], 0.0)
-        nc.scalar.activation(out=warm[:, 1:2], in_=warm[:, 0:1], func=ACTF.Square)
+        idle_plain = psum.tile([P, P], F32, name="idle_plain", tag="acc1")
 
-        codes = {}
-        planes = {}
-        for r in range(5):
-            codes[r] = keep.tile([P, PASSES * P], U32, name="codes%d" % r, align_bytes=64)
-            planes[r] = keep.tile([P, PASSES * P], U8, name="planes%d" % r, align_bytes=64)
+        w_codes = keep.tile([P, PASSES * P], U32, name="w_codes", align_bytes=64)
+        w_plane = keep.tile([P, PASSES * P], U8, name="w_plane", align_bytes=64)
+        x_codes = keep.tile([P, B_TILES * PASSES * P], U32, name="x_codes", align_bytes=64)
+        x_plane = keep.tile([P, B_TILES * PASSES * P], U8, name="x_plane", align_bytes=64)
 
         groups = {}
-        row_units = {}
-        for r in range(5):
-            plan = GROUPS_LAST if r == 4 else GROUPS
-            row_units[r] = []
+        units = {"w": [], "x": []}
+        for which, sizes_list in (
+            ("w", [[2, 2]] * 4 + [[2]]),
+            ("x", [[2, 2]] * 17 + [[2], [1, 1]]),
+        ):
             p0 = 0
-            for gi, sizes in enumerate(plan):
-                groups[(r, gi)] = [p0, sum(sizes), 0, 1]
+            for gi, sizes in enumerate(sizes_list):
+                groups[(which, gi)] = [p0, sum(sizes), 0, 1]
                 off = 0
                 for np_ in sizes:
-                    row_units[r].append(("B", r, p0 + off, np_, (r, gi), off))
+                    units[which].append(("B", which, p0 + off, np_, (which, gi), off))
                     off += np_
                 p0 += off
-        order = [("A", 0), ("A", 1), ("A", 2)]
-        for w in range(9):
-            order.append(row_units[0][w])
-            if w + 3 < 9:
-                order.append(("A", w + 3))
-        for r in range(1, 5):
-            order.extend(row_units[r])
+        order = [("A", g) for g in range(9)]
+        order.extend(units["w"])
+        x_start = len(order)
+        order.extend(units["x"])
         n_units = len(order)
-        last_index = {}
         for i, unit in enumerate(order):
             if unit[0] == "B":
                 groups[unit[4]][2] = i
-                last_index[unit[1]] = i
-        groups[(4, len(GROUPS_LAST) - 1)][3] = 0
+        groups[("x", 18)][3] = 0
 
         q_at = {}
         for key in sorted(groups):
             g = groups[key]
             step = g[2] + 1 + g[3]
             q_at[step] = q_at.get(step, []) + [key]
+        total = B_TILES * PASSES
         mx_pre = {}
         mx_post = {}
+        for m in range(7):
+            mx_pre[x_start + PERIOD * (m + 1) + PERIOD - 1] = (2 * PERIOD * m, 2 * PERIOD * (m + 1))
+        mx_pre[n_units] = (2 * PERIOD * 7, total - 2)
+        mx_post[n_units] = (total - 2, total)
         sq_a = {}
         sq_b = {}
         sq_c = {}
-        for r in range(1, 4):
-            s = last_index[r] + MX_LAG
-            mx_pre[s] = (r, 0, PASSES)
-            sq_a[s + 2] = r
-            sq_b[s + 3] = r
-            sq_c[s + 4] = r
-        mx_pre[n_units] = (4, 0, PASSES - 2)
-        mx_post[n_units] = (4, PASSES - 2, PASSES)
-        sq_a[n_units] = 4
-        sq_b[n_units] = 4
-        sq_c[n_units] = 4
+        for step in sorted(mx_pre):
+            g0, g1 = mx_pre[step]
+            for r in range(B_TILES - 1):
+                if g0 <= r * PASSES + PASSES - 1 < g1:
+                    sq_a[step + 2] = r
+                    sq_b[step + 3] = r
+                    sq_c[step + 4] = r
+        sq_a[n_units] = B_TILES - 1
+        sq_b[n_units] = B_TILES - 1
+        sq_c[n_units] = B_TILES - 1
 
-        def on_vector(unit, i):
+        def on_vector(unit):
             if unit[0] == "A":
                 return unit[1] % 2 == 1
-            r, p0 = unit[1], unit[2]
-            if r == 0:
-                return p0 in (2, 8, 14)
-            if r == 4 and p0 == PASSES - 1:
+            which, p0 = unit[1], unit[2]
+            if which == "w":
+                return p0 in (2, 6, 10, 14)
+            if p0 == total - 1:
                 return True
-            return p0 == 8
+            return (p0 // 2) % PERIOD == 2 and p0 // 2 != 34
 
         banks = {}
         s_tiles = {}
@@ -142,17 +142,17 @@ def tile_digitcaps_kernel(tc, x, W, out):
         sq = {}
         c_inv = 1.0 / 1152.0
 
-        def run_mx(r, g0, g1):
-            if g0 == 0:
-                acc[r] = psum.tile([P, N], F32, name="acc%d" % (r % 2), tag="acc%d" % (r % 2))
-            for g in range(g0, g1):
-                cols = slice(g * P, (g + 1) * P)
+        def run_mx(g0, g1):
+            for gg in range(g0, g1):
+                r, g = gg // PASSES, gg % PASSES
+                if g == 0:
+                    acc[r] = psum.tile([P, N], F32, name="acc%d" % (r % 2), tag="acc%d" % (r % 2))
                 nc.tensor.matmul_mx(
                     out=acc[r][:],
-                    lhsT=codes[r][:, cols].bitcast(FP8X4),
-                    lhsT_scale=planes[r][:, cols],
-                    rhs=codes[0][:, cols].bitcast(FP8X4),
-                    rhs_scale=planes[0][:, cols],
+                    lhsT=x_codes[:, gg * P : (gg + 1) * P].bitcast(FP8X4),
+                    lhsT_scale=x_plane[:, gg * P : (gg + 1) * P],
+                    rhs=w_codes[:, g * P : (g + 1) * P].bitcast(FP8X4),
+                    rhs_scale=w_plane[:, g * P : (g + 1) * P],
                     start=(g == 0),
                     stop=(g == PASSES - 1),
                 )
@@ -168,14 +168,16 @@ def tile_digitcaps_kernel(tc, x, W, out):
                             out=ps[:, e * P : (e + 1) * P], in_=w_words[unit[1]][:, :, e], identity=ident[:]
                         )
                 else:
-                    r, p0, np_ = unit[1], unit[2], unit[3]
+                    which, p0, np_ = unit[1], unit[2], unit[3]
                     for i in range(2 * np_):
-                        if r == 0:
+                        if which == "w":
                             src = s_tiles[p0 // 2][:, i * P : (i + 1) * P]
                         else:
-                            words, off = src_words[(r, p0 + i // 2)]
+                            words, off = x_words[p0 + i // 2]
                             src = words[:, off + (i % 2) * P : off + (i % 2 + 1) * P]
                         nc.tensor.transpose(out=ps[:, i * P : (i + 1) * P], in_=src, identity=ident[:])
+                for i in range(IDLE_AFTER.get(step, 0)):
+                    nc.tensor.matmul(out=idle_plain[:], lhsT=zeros[:], rhs=zeros[:], start=True, stop=True)
             if step in mx_pre:
                 run_mx(*mx_pre[step])
             if step >= 1:
@@ -189,21 +191,23 @@ def tile_digitcaps_kernel(tc, x, W, out):
                 else:
                     np_, key, off = unit[3], unit[4], unit[5]
                     if off == 0:
-                        grouped[key] = stage.tile([P, groups[key][1] * 512], BF16, name="grp", tag="grp", align_bytes=64)
+                        grouped[key] = stage.tile(
+                            [P, groups[key][1] * 512], BF16, name="grp", tag="grp", align_bytes=64
+                        )
                     dst = grouped[key][:].bitcast(F32)[:, off * 256 : (off + np_) * 256].rearrange(
                         "q (c b u) -> q c b u", c=np_, u=2
                     )
                     src = ps[:, 0 : np_ * 256].rearrange("q (c u b) -> q c b u", c=np_, u=2)
-                if on_vector(unit, step - 1):
+                if on_vector(unit):
                     nc.vector.tensor_copy(out=dst, in_=src)
                 else:
                     nc.scalar.copy(out=dst, in_=src)
             for key in q_at.get(step, []):
                 p0, np_ = groups[key][0], groups[key][1]
-                cols = slice(p0 * P, (p0 + np_) * P)
+                cd, pl = (w_codes, w_plane) if key[0] == "w" else (x_codes, x_plane)
                 nc.vector.quantize_mx(
-                    out=codes[key[0]][:, cols].bitcast(FP8X4),
-                    scales=planes[key[0]][:, cols],
+                    out=cd[:, p0 * P : (p0 + np_) * P].bitcast(FP8X4),
+                    scales=pl[:, p0 * P : (p0 + np_) * P],
                     in_=grouped[key][:],
                 )
             if step in mx_post:
@@ -211,23 +215,24 @@ def tile_digitcaps_kernel(tc, x, W, out):
             if step in sq_a:
                 r = sq_a[step]
                 q = small.tile([P, N], F32, name="q")
-                a = small.tile([P, N], F32, name="a")
+                rs = small.tile([P, N], F32, name="rs")
                 nc.scalar.activation(out=q[:], in_=acc[r][:], func=ACTF.Square, scale=c_inv)
-                nc.scalar.activation(out=a[:], in_=acc[r][:], func=ACTF.Abs, scale=c_inv)
-                sq[r] = [q, a]
+                nc.scalar.activation(out=rs[:], in_=q[:], func=ACTF.Abs_reciprocal_sqrt, bias=1.0)
+                sq[r] = [rs]
             if step in sq_b:
                 r = sq_b[step]
-                den = small.tile([P, N], F32, name="den")
-                rec = small.tile([P, N], F32, name="rec")
-                nc.vector.tensor_scalar_add(out=den[:], in0=sq[r][0][:], scalar1=1.0)
-                nc.vector.reciprocal(out=rec[:], in_=den[:])
-                sq[r].append(rec)
+                z = small.tile([P, N], F32, name="z")
+                nc.vector.scalar_tensor_tensor(
+                    out=z[:], in0=acc[r][:], scalar=c_inv, in1=sq[r][0][:], op0=ALU.mult, op1=ALU.mult
+                )
+                sq[r].append(z)
             if step in sq_c:
                 r = sq_c[step]
-                t = small.tile([P, N], F32, name="t")
+                z = sq[r][1]
+                az = small.tile([P, N], F32, name="az")
                 v = small.tile([P, N], F32, name="v")
                 nc.vector.scalar_tensor_tensor(
-                    out=t[:], in0=acc[r][:], scalar=c_inv, in1=sq[r][2][:], op0=ALU.mult, op1=ALU.mult
+                    out=az[:], in0=z[:], scalar=-1.0, in1=z[:], op0=ALU.mult, op1=ALU.max
                 )
-                nc.vector.tensor_tensor(out=v[:], in0=t[:], in1=sq[r][1][:], op=ALU.mult)
-                nc.sync.dma_start(out=out_rows[(r - 1) * P : r * P, :], in_=v[:])
+                nc.vector.tensor_tensor(out=v[:], in0=az[:], in1=z[:], op=ALU.mult)
+                nc.sync.dma_start(out=out_rows[r * P : (r + 1) * P, :], in_=v[:])

@@ -23,8 +23,7 @@ W_CHUNKS = [(0, 1), (1, 2), (2, 3), (3, 4), (4, 5), (5, 6), (6, 7), (7, 8), (8, 
 X_CHUNKS = [(0, 6), (6, 12), (12, 18)]
 X_CHUNKS_LAST = [(0, 6), (6, 12), (12, 16), (16, 18)]
 BANKS = 6
-PERIOD = 4
-IDLE_AFTER = {8: 4, 12: 1, 16: 1, 21: 1}
+MX_RUNS = [(9, 0, 4), (14, 4, 9), (18, 9, 13), (23, 13, 18), (27, 18, 22), (32, 22, 27)]
 
 
 def tile_digitcaps_kernel(tc, x, W, out):
@@ -61,14 +60,11 @@ def tile_digitcaps_kernel(tc, x, W, out):
                 for g in range(p0, p1):
                     x_words[r * PASSES + g] = (words, (g - p0) * 256)
 
-        zeros = keep.tile([P, P], F32, name="zeros")
         warm = keep.tile([P, 2], F32, name="warm")
-        nc.vector.memset(zeros[:], 0.0)
         nc.vector.memset(warm[:], 1.0)
         nc.scalar.activation(out=warm[:, 1:2], in_=warm[:, 0:1], func=ACTF.Abs_reciprocal_sqrt)
         ident = keep.tile([P, P], F32, name="ident")
         make_identity(nc, ident[:])
-        idle_plain = psum.tile([P, P], F32, name="idle_plain", tag="acc1")
 
         w_codes = keep.tile([P, PASSES * P], U32, name="w_codes", align_bytes=64)
         w_plane = keep.tile([P, PASSES * P], U8, name="w_plane", align_bytes=64)
@@ -89,8 +85,11 @@ def tile_digitcaps_kernel(tc, x, W, out):
                     units[which].append(("B", which, p0 + off, np_, (which, gi), off))
                     off += np_
                 p0 += off
-        order = [("A", g) for g in range(9)]
-        order.extend(units["w"])
+        order = [("A", 0), ("A", 1), ("A", 2)]
+        for w in range(9):
+            order.append(units["w"][w])
+            if w + 3 < 9:
+                order.append(("A", w + 3))
         x_start = len(order)
         order.extend(units["x"])
         n_units = len(order)
@@ -107,9 +106,9 @@ def tile_digitcaps_kernel(tc, x, W, out):
         total = B_TILES * PASSES
         mx_pre = {}
         mx_post = {}
-        for m in range(7):
-            mx_pre[x_start + PERIOD * (m + 1) + PERIOD - 1] = (2 * PERIOD * m, 2 * PERIOD * (m + 1))
-        mx_pre[n_units] = (2 * PERIOD * 7, total - 2)
+        for after, u0, u1 in MX_RUNS:
+            mx_pre[x_start + after] = (2 * u0, 2 * u1)
+        mx_pre[n_units] = (2 * MX_RUNS[-1][2], total - 2)
         mx_post[n_units] = (total - 2, total)
         sq_a = {}
         sq_b = {}
@@ -133,7 +132,7 @@ def tile_digitcaps_kernel(tc, x, W, out):
                 return p0 in (2, 6, 10, 14)
             if p0 == total - 1:
                 return True
-            return (p0 // 2) % PERIOD == 2 and p0 // 2 != 34
+            return (p0 // 2) % 4 == 2 and p0 // 2 != 34
 
         banks = {}
         s_tiles = {}
@@ -176,8 +175,6 @@ def tile_digitcaps_kernel(tc, x, W, out):
                             words, off = x_words[p0 + i // 2]
                             src = words[:, off + (i % 2) * P : off + (i % 2 + 1) * P]
                         nc.tensor.transpose(out=ps[:, i * P : (i + 1) * P], in_=src, identity=ident[:])
-                for i in range(IDLE_AFTER.get(step, 0)):
-                    nc.tensor.matmul(out=idle_plain[:], lhsT=zeros[:], rhs=zeros[:], start=True, stop=True)
             if step in mx_pre:
                 run_mx(*mx_pre[step])
             if step >= 1:

@@ -23,7 +23,7 @@ W_CHUNKS = [(0, 1), (1, 2), (2, 3), (3, 4), (4, 5), (5, 6), (6, 7), (7, 8), (8, 
 X_CHUNKS = [(0, 6), (6, 12), (12, 18)]
 X_CHUNKS_LAST = [(0, 6), (6, 12), (12, 16), (16, 18)]
 BANKS = 6
-MX_RUNS = [(9, 0, 4), (14, 4, 9), (18, 9, 13), (23, 13, 18), (27, 18, 22), (32, 22, 27)]
+MX_RUNS = [(9, 0, 4), (14, 4, 9), (18, 9, 13), (23, 13, 18), (27, 18, 22)]
 
 
 def tile_digitcaps_kernel(tc, x, W, out):
@@ -105,24 +105,23 @@ def tile_digitcaps_kernel(tc, x, W, out):
             q_at[step] = q_at.get(step, []) + [key]
         total = B_TILES * PASSES
         mx_pre = {}
-        mx_post = {}
         for after, u0, u1 in MX_RUNS:
             mx_pre[x_start + after] = (2 * u0, 2 * u1)
         mx_pre[n_units] = (2 * MX_RUNS[-1][2], total - 2)
-        mx_post[n_units] = (total - 2, total)
         sq_a = {}
         sq_b = {}
         sq_c = {}
+        late = []
         for step in sorted(mx_pre):
             g0, g1 = mx_pre[step]
             for r in range(B_TILES - 1):
                 if g0 <= r * PASSES + PASSES - 1 < g1:
-                    sq_a[step + 2] = r
-                    sq_b[step + 3] = r
-                    sq_c[step + 4] = r
-        sq_a[n_units] = B_TILES - 1
-        sq_b[n_units] = B_TILES - 1
-        sq_c[n_units] = B_TILES - 1
+                    if step == n_units:
+                        late.append(r)
+                    else:
+                        sq_a[step + 2] = r
+                        sq_b[step + 3] = r
+                        sq_c[step + 4] = r
 
         def on_vector(unit):
             if unit[0] == "A":
@@ -155,6 +154,30 @@ def tile_digitcaps_kernel(tc, x, W, out):
                     start=(g == 0),
                     stop=(g == PASSES - 1),
                 )
+
+        def squash_a(r):
+            q = small.tile([P, N], F32, name="q")
+            rs = small.tile([P, N], F32, name="rs")
+            nc.scalar.activation(out=q[:], in_=acc[r][:], func=ACTF.Square, scale=c_inv)
+            nc.scalar.activation(out=rs[:], in_=q[:], func=ACTF.Abs_reciprocal_sqrt, bias=1.0)
+            sq[r] = [rs]
+
+        def squash_b(r):
+            z = small.tile([P, N], F32, name="z")
+            nc.vector.scalar_tensor_tensor(
+                out=z[:], in0=acc[r][:], scalar=c_inv, in1=sq[r][0][:], op0=ALU.mult, op1=ALU.mult
+            )
+            sq[r].append(z)
+
+        def squash_c(r):
+            z = sq[r][1]
+            az = small.tile([P, N], F32, name="az")
+            v = small.tile([P, N], F32, name="v")
+            nc.vector.scalar_tensor_tensor(
+                out=az[:], in0=z[:], scalar=-1.0, in1=z[:], op0=ALU.mult, op1=ALU.max
+            )
+            nc.vector.tensor_tensor(out=v[:], in0=az[:], in1=z[:], op=ALU.mult)
+            nc.sync.dma_start(out=out_rows[r * P : (r + 1) * P, :], in_=v[:])
 
         for step in range(n_units + 1):
             if step < n_units:
@@ -207,29 +230,17 @@ def tile_digitcaps_kernel(tc, x, W, out):
                     scales=pl[:, p0 * P : (p0 + np_) * P],
                     in_=grouped[key][:],
                 )
-            if step in mx_post:
-                run_mx(*mx_post[step])
             if step in sq_a:
-                r = sq_a[step]
-                q = small.tile([P, N], F32, name="q")
-                rs = small.tile([P, N], F32, name="rs")
-                nc.scalar.activation(out=q[:], in_=acc[r][:], func=ACTF.Square, scale=c_inv)
-                nc.scalar.activation(out=rs[:], in_=q[:], func=ACTF.Abs_reciprocal_sqrt, bias=1.0)
-                sq[r] = [rs]
+                squash_a(sq_a[step])
             if step in sq_b:
-                r = sq_b[step]
-                z = small.tile([P, N], F32, name="z")
-                nc.vector.scalar_tensor_tensor(
-                    out=z[:], in0=acc[r][:], scalar=c_inv, in1=sq[r][0][:], op0=ALU.mult, op1=ALU.mult
-                )
-                sq[r].append(z)
+                squash_b(sq_b[step])
             if step in sq_c:
-                r = sq_c[step]
-                z = sq[r][1]
-                az = small.tile([P, N], F32, name="az")
-                v = small.tile([P, N], F32, name="v")
-                nc.vector.scalar_tensor_tensor(
-                    out=az[:], in0=z[:], scalar=-1.0, in1=z[:], op0=ALU.mult, op1=ALU.max
-                )
-                nc.vector.tensor_tensor(out=v[:], in0=az[:], in1=z[:], op=ALU.mult)
-                nc.sync.dma_start(out=out_rows[r * P : (r + 1) * P, :], in_=v[:])
+                squash_c(sq_c[step])
+        for r in late:
+            squash_a(r)
+            squash_b(r)
+            squash_c(r)
+        run_mx(total - 2, total)
+        squash_a(B_TILES - 1)
+        squash_b(B_TILES - 1)
+        squash_c(B_TILES - 1)

@@ -15,15 +15,21 @@ P = 128
 BS = 512
 K = 9216
 N = 128
-PASSES = K // 512
+PAIRS = K // 1024
 B_TILES = BS // P
 FLOPS = 2 * BS * K * N
-
-W_CHUNKS = [(0, 1), (1, 2), (2, 3), (3, 4), (4, 5), (5, 6), (6, 7), (7, 8), (8, 9)]
-X_CHUNKS = [(0, 6), (6, 12), (12, 18)]
-X_CHUNKS_LAST = [(0, 6), (6, 12), (12, 16), (16, 18)]
 BANKS = 6
-MX_RUNS = [(9, 0, 4), (14, 4, 9), (18, 9, 13), (23, 13, 18), (27, 18, 22)]
+C_INV = 1.0 / 1152.0
+
+def on_vector(unit):
+    kind, r, g = unit
+    if kind == "A":
+        return g % 2 == 1
+    if kind == "W":
+        return g % 2 == 0
+    if r >= 2:
+        return g % 4 == 2
+    return False
 
 
 def tile_digitcaps_kernel(tc, x, W, out):
@@ -34,31 +40,73 @@ def tile_digitcaps_kernel(tc, x, W, out):
 
     with ExitStack() as ctx:
         keep = ctx.enter_context(tc.tile_pool(name="keep", bufs=1))
-        stage = ctx.enter_context(tc.tile_pool(name="stage", bufs=4))
+        stage = ctx.enter_context(tc.tile_pool(name="stage", bufs=6))
         small = ctx.enter_context(tc.tile_pool(name="small", bufs=2))
         psum = ctx.enter_context(tc.psum_pool(name="psum", bufs=1))
         ctx.enter_context(tc.manual_schedule())
 
+        order = []
+        loads = []
+        for g in range(PAIRS):
+            loads.append(("W", 0, g, g + 1))
+            if g == 0:
+                loads.append(("W", 0, 1, 2))
+            elif g + 1 < PAIRS:
+                loads[-1] = ("W", 0, g + 1, g + 2)
+            else:
+                loads.pop()
+            loads.append(("X", 0, g, g + 1))
+            loads.append(("X", 1, g, g + 1))
+        for r in (2, 3):
+            loads.extend([("X", r, 0, 3), ("X", r, 3, 6), ("X", r, 6, 8), ("X", r, 8, 9)])
+        order.append(("A", 0, 0))
+        for g in range(PAIRS):
+            if g + 1 < PAIRS:
+                order.append(("A", 0, g + 1))
+            order.append(("X", 0, g))
+            order.append(("W", 0, g))
+            order.append(("X", 1, g))
+        n_first = len(order)
+        for r in (2, 3):
+            for g in range(PAIRS):
+                order.append(("X", r, g))
+
+        groups = []
+        for g in range(PAIRS):
+            groups.append([("W", 0, g)])
+            groups.append([("X", 0, g), ("X", 1, g)])
+        for r in (2, 3):
+            for g in range(0, PAIRS - 1, 2):
+                groups.append([("X", r, g), ("X", r, g + 1)])
+            groups.append([("X", r, PAIRS - 1)])
+
+        def q_lag(members):
+            return 0 if members[0] == ("X", 3, PAIRS - 1) else 1
+
+        mx_at = {}
+        for g in range(1, PAIRS, 2):
+            mx_at[4 * g + 4 + 5] = [(0, g - 1), (1, g - 1), (0, g), (1, g)]
+        mx_at[n_first + 5] = [(0, 8), (1, 8)]
+        mx_at[n_first + 11] = [(2, g) for g in range(6)]
+        sq_at = {n_first + 7: [0], n_first + 9: [1]}
+
+
         w_words = {}
-        for k, (g0, g1) in enumerate(W_CHUNKS):
-            wp = keep.tile([P, (g1 - g0) * 1024], BF16, name="wp%d" % k)
-            nc.sync.dma_start(
-                out=wp[:].rearrange("q (g f) -> q g f", f=1024), in_=w_rows[:, g0:g1, :]
-            )
-            words = wp[:].bitcast(F32)
-            for g in range(g0, g1):
-                w_words[g] = words[:, (g - g0) * 512 : (g - g0 + 1) * 512].rearrange(
-                    "q (n e) -> q n e", e=4
-                )
         x_words = {}
-        for r in range(B_TILES):
-            chunks = X_CHUNKS_LAST if r == B_TILES - 1 else X_CHUNKS
-            for k, (p0, p1) in enumerate(chunks):
-                xt = keep.tile([P, (p1 - p0) * 512], BF16, name="x%d_%d" % (r, k))
-                nc.sync.dma_start(out=xt[:], in_=x_rows[r * P : (r + 1) * P, p0 * 512 : p1 * 512])
-                words = xt[:].bitcast(F32)
-                for g in range(p0, p1):
-                    x_words[r * PASSES + g] = (words, (g - p0) * 256)
+        for load in loads:
+            kind, r, g0, g1 = load
+            t = keep.tile([P, (g1 - g0) * 1024], BF16, name="ld%s%d_%d" % (kind, r, g0))
+            words = t[:].bitcast(F32)
+            if kind == "W":
+                nc.sync.dma_start(out=t[:].rearrange("q (g f) -> q g f", f=1024), in_=w_rows[:, g0:g1, :])
+            else:
+                nc.sync.dma_start(out=t[:], in_=x_rows[r * P : (r + 1) * P, g0 * 1024 : g1 * 1024])
+            for g in range(g0, g1):
+                piece = words[:, (g - g0) * 512 : (g - g0 + 1) * 512]
+                if kind == "W":
+                    w_words[g] = piece.rearrange("q (n e) -> q n e", e=4)
+                else:
+                    x_words[(r, g)] = piece
 
         warm = keep.tile([P, 2], F32, name="warm")
         nc.vector.memset(warm[:], 1.0)
@@ -66,106 +114,88 @@ def tile_digitcaps_kernel(tc, x, W, out):
         ident = keep.tile([P, P], F32, name="ident")
         make_identity(nc, ident[:])
 
-        w_codes = keep.tile([P, PASSES * P], U32, name="w_codes", align_bytes=64)
-        w_plane = keep.tile([P, PASSES * P], U8, name="w_plane", align_bytes=64)
-        x_codes = keep.tile([P, B_TILES * PASSES * P], U32, name="x_codes", align_bytes=64)
-        x_plane = keep.tile([P, B_TILES * PASSES * P], U8, name="x_plane", align_bytes=64)
+        group_of = {}
+        for members in groups:
+            codes = keep.tile([P, 256 * len(members)], U32, name="c%s%d_%d" % members[0], align_bytes=64)
+            plane = keep.tile([P, 256 * len(members)], U8, name="p%s%d_%d" % members[0], align_bytes=64)
+            entry = [members, codes, plane, None]
+            for unit in members:
+                group_of[unit] = entry
 
-        groups = {}
-        units = {"w": [], "x": []}
-        for which, sizes_list in (
-            ("w", [[2, 2]] * 4 + [[2]]),
-            ("x", [[2, 2]] * 17 + [[2], [1, 1]]),
-        ):
-            p0 = 0
-            for gi, sizes in enumerate(sizes_list):
-                groups[(which, gi)] = [p0, sum(sizes), 0, 1]
-                off = 0
-                for np_ in sizes:
-                    units[which].append(("B", which, p0 + off, np_, (which, gi), off))
-                    off += np_
-                p0 += off
-        order = [("A", 0), ("A", 1), ("A", 2)]
-        for w in range(9):
-            order.append(units["w"][w])
-            if w + 3 < 9:
-                order.append(("A", w + 3))
-        x_start = len(order)
-        order.extend(units["x"])
-        n_units = len(order)
+        def operand(unit, half):
+            entry = group_of[unit]
+            c0 = (2 * entry[0].index(unit) + half) * P
+            return entry[1][:, c0 : c0 + P].bitcast(FP8X4), entry[2][:, c0 : c0 + P]
+
+        pos = {}
         for i, unit in enumerate(order):
-            if unit[0] == "B":
-                groups[unit[4]][2] = i
-        groups[("x", 18)][3] = 0
-
+            pos[unit] = i
         q_at = {}
-        for key in sorted(groups):
-            g = groups[key]
-            step = g[2] + 1 + g[3]
-            q_at[step] = q_at.get(step, []) + [key]
-        total = B_TILES * PASSES
-        mx_pre = {}
-        for after, u0, u1 in MX_RUNS:
-            mx_pre[x_start + after] = (2 * u0, 2 * u1)
-        mx_pre[n_units] = (2 * MX_RUNS[-1][2], total - 2)
-        sq_a = {}
-        sq_b = {}
-        sq_c = {}
-        late = []
-        for step in sorted(mx_pre):
-            g0, g1 = mx_pre[step]
-            for r in range(B_TILES - 1):
-                if g0 <= r * PASSES + PASSES - 1 < g1:
-                    if step == n_units:
-                        late.append(r)
-                    else:
-                        sq_a[step + 2] = r
-                        sq_b[step + 3] = r
-                        sq_c[step + 4] = r
+        for members in groups:
+            step = max(pos[u] for u in members) + 1 + q_lag(members)
+            q_at.setdefault(step, []).append(members)
 
-        def on_vector(unit):
-            if unit[0] == "A":
-                return unit[1] % 2 == 1
-            which, p0 = unit[1], unit[2]
-            if which == "w":
-                return p0 in (2, 6, 10, 14)
-            if p0 == total - 1:
-                return True
-            return (p0 // 2) % 4 == 2 and p0 // 2 != 34
-
-        banks = {}
-        s_tiles = {}
-        grouped = {}
         acc = {}
         sq = {}
-        c_inv = 1.0 / 1152.0
+        s_tiles = {}
 
-        def run_mx(g0, g1):
-            for gg in range(g0, g1):
-                r, g = gg // PASSES, gg % PASSES
-                if g == 0:
-                    acc[r] = psum.tile([P, N], F32, name="acc%d" % (r % 2), tag="acc%d" % (r % 2))
+        def transposes(unit, ps):
+            kind, r, g = unit
+            for i in range(4):
+                if kind == "A":
+                    src = w_words[g][:, :, i]
+                elif kind == "W":
+                    src = s_tiles[g][:, i * P : (i + 1) * P]
+                else:
+                    src = x_words[(r, g)][:, i * P : (i + 1) * P]
+                nc.tensor.transpose(out=ps[:, i * P : (i + 1) * P], in_=src, identity=ident[:])
+
+        def evacuate(unit, ps):
+            kind, r, g = unit
+            if kind == "A":
+                s_tiles[g] = keep.tile([P, 512], F32, name="s%d" % g)
+                dst = s_tiles[g][:].rearrange("n (p e) -> n p e", e=4)
+                src = ps[:].rearrange("n (e p) -> n p e", e=4)
+            else:
+                entry = group_of[unit]
+                members = entry[0]
+                if entry[3] is None:
+                    tag = "grp%d" % len(members)
+                    entry[3] = stage.tile([P, 1024 * len(members)], BF16, name=tag, tag=tag, align_bytes=64)
+                off = members.index(unit) * 512
+                dst = entry[3][:].bitcast(F32)[:, off : off + 512].rearrange("q (c b u) -> q c b u", c=2, u=2)
+                src = ps[:].rearrange("q (c u b) -> q c b u", c=2, u=2)
+            if on_vector(unit):
+                nc.vector.tensor_copy(out=dst, in_=src)
+            else:
+                nc.scalar.copy(out=dst, in_=src)
+
+        def quantize(members):
+            entry = group_of[members[0]]
+            nc.vector.quantize_mx(out=entry[1][:].bitcast(FP8X4), scales=entry[2][:], in_=entry[3][:])
+
+        def run_mx(r, g):
+            if g == 0:
+                acc[r] = psum.tile([P, N], F32, name="acc%d" % (r % 2), tag="acc%d" % (r % 2))
+            for half in range(2):
+                xc, xp = operand(("X", r, g), half)
+                wc, wp = operand(("W", 0, g), half)
                 nc.tensor.matmul_mx(
-                    out=acc[r][:],
-                    lhsT=x_codes[:, gg * P : (gg + 1) * P].bitcast(FP8X4),
-                    lhsT_scale=x_plane[:, gg * P : (gg + 1) * P],
-                    rhs=w_codes[:, g * P : (g + 1) * P].bitcast(FP8X4),
-                    rhs_scale=w_plane[:, g * P : (g + 1) * P],
-                    start=(g == 0),
-                    stop=(g == PASSES - 1),
+                    out=acc[r][:], lhsT=xc, lhsT_scale=xp, rhs=wc, rhs_scale=wp,
+                    start=(g == 0 and half == 0), stop=(g == PAIRS - 1 and half == 1),
                 )
 
         def squash_a(r):
             q = small.tile([P, N], F32, name="q")
             rs = small.tile([P, N], F32, name="rs")
-            nc.scalar.activation(out=q[:], in_=acc[r][:], func=ACTF.Square, scale=c_inv)
+            nc.scalar.activation(out=q[:], in_=acc[r][:], func=ACTF.Square, scale=C_INV)
             nc.scalar.activation(out=rs[:], in_=q[:], func=ACTF.Abs_reciprocal_sqrt, bias=1.0)
             sq[r] = [rs]
 
         def squash_b(r):
             z = small.tile([P, N], F32, name="z")
             nc.vector.scalar_tensor_tensor(
-                out=z[:], in0=acc[r][:], scalar=c_inv, in1=sq[r][0][:], op0=ALU.mult, op1=ALU.mult
+                out=z[:], in0=acc[r][:], scalar=C_INV, in1=sq[r][0][:], op0=ALU.mult, op1=ALU.mult
             )
             sq[r].append(z)
 
@@ -179,68 +209,32 @@ def tile_digitcaps_kernel(tc, x, W, out):
             nc.vector.tensor_tensor(out=v[:], in0=az[:], in1=z[:], op=ALU.mult)
             nc.sync.dma_start(out=out_rows[r * P : (r + 1) * P, :], in_=v[:])
 
-        for step in range(n_units + 1):
+        banks = {}
+        n_units = len(order)
+        for step in range(n_units + 3):
             if step < n_units:
-                unit = order[step]
                 ps = psum.tile([P, 512], F32, name="tp%d" % (step % BANKS), tag="tp%d" % (step % BANKS))
                 banks[step] = ps
-                if unit[0] == "A":
-                    for e in range(4):
-                        nc.tensor.transpose(
-                            out=ps[:, e * P : (e + 1) * P], in_=w_words[unit[1]][:, :, e], identity=ident[:]
-                        )
-                else:
-                    which, p0, np_ = unit[1], unit[2], unit[3]
-                    for i in range(2 * np_):
-                        if which == "w":
-                            src = s_tiles[p0 // 2][:, i * P : (i + 1) * P]
-                        else:
-                            words, off = x_words[p0 + i // 2]
-                            src = words[:, off + (i % 2) * P : off + (i % 2 + 1) * P]
-                        nc.tensor.transpose(out=ps[:, i * P : (i + 1) * P], in_=src, identity=ident[:])
-            if step in mx_pre:
-                run_mx(*mx_pre[step])
-            if step >= 1:
-                unit = order[step - 1]
-                ps = banks[step - 1]
-                if unit[0] == "A":
-                    st = keep.tile([P, 512], F32, name="s%d" % unit[1])
-                    s_tiles[unit[1]] = st
-                    dst = st[:].rearrange("n (p e) -> n p e", e=4)
-                    src = ps[:].rearrange("n (e p) -> n p e", e=4)
-                else:
-                    np_, key, off = unit[3], unit[4], unit[5]
-                    if off == 0:
-                        grouped[key] = stage.tile(
-                            [P, groups[key][1] * 512], BF16, name="grp", tag="grp", align_bytes=64
-                        )
-                    dst = grouped[key][:].bitcast(F32)[:, off * 256 : (off + np_) * 256].rearrange(
-                        "q (c b u) -> q c b u", c=np_, u=2
-                    )
-                    src = ps[:, 0 : np_ * 256].rearrange("q (c u b) -> q c b u", c=np_, u=2)
-                if on_vector(unit):
-                    nc.vector.tensor_copy(out=dst, in_=src)
-                else:
-                    nc.scalar.copy(out=dst, in_=src)
-            for key in q_at.get(step, []):
-                p0, np_ = groups[key][0], groups[key][1]
-                cd, pl = (w_codes, w_plane) if key[0] == "w" else (x_codes, x_plane)
-                nc.vector.quantize_mx(
-                    out=cd[:, p0 * P : (p0 + np_) * P].bitcast(FP8X4),
-                    scales=pl[:, p0 * P : (p0 + np_) * P],
-                    in_=grouped[key][:],
-                )
-            if step in sq_a:
-                squash_a(sq_a[step])
-            if step in sq_b:
-                squash_b(sq_b[step])
-            if step in sq_c:
-                squash_c(sq_c[step])
-        for r in late:
-            squash_a(r)
-            squash_b(r)
-            squash_c(r)
-        run_mx(total - 2, total)
-        squash_a(B_TILES - 1)
-        squash_b(B_TILES - 1)
-        squash_c(B_TILES - 1)
+                transposes(order[step], ps)
+            for r, g in mx_at.get(step, []):
+                run_mx(r, g)
+            if 1 <= step <= n_units:
+                evacuate(order[step - 1], banks[step - 1])
+            for members in q_at.get(step, []):
+                quantize(members)
+            for r in sq_at.get(step, []):
+                squash_a(r)
+            for r in sq_at.get(step - 1, []):
+                squash_b(r)
+            for r in sq_at.get(step - 2, []):
+                squash_c(r)
+        for g in range(6, PAIRS):
+            run_mx(2, g)
+        for g in range(0, PAIRS):
+            run_mx(3, g)
+        squash_a(2)
+        squash_b(2)
+        squash_c(2)
+        squash_a(3)
+        squash_b(3)
+        squash_c(3)

@@ -15,99 +15,113 @@ P = 128
 BS = 512
 K = 9216
 N = 128
-PAIRS = K // 1024
+PASSES = K // 512
+PAIRS = PASSES // 2
 B_TILES = BS // P
 FLOPS = 2 * BS * K * N
 BANKS = 6
 C_INV = 1.0 / 1152.0
 
-def on_vector(unit):
-    kind, r, g = unit
-    if kind == "A":
-        return g % 2 == 1
-    if kind == "W":
-        return g % 2 == 0
-    if r >= 2:
-        return g % 4 == 2
-    return False
+RUN = 6
+RUN_MAX = 10
+LAG = 5
+HOLD = 4
+IDLE = {9: [512,512,512], 14: [512], 18: [512]}
 
 
 def tile_digitcaps_kernel(tc, x, W, out):
     nc = tc.nc
-    x_rows = x.rearrange("b p e -> b (p e)")
+    x_rows = x.rearrange("(r q) p e -> q r (p e)", q=P)
     w_rows = W.rearrange("o (g q) c d e -> q (o g) (c d e)", q=P)
     out_rows = out.rearrange("b c d o -> b (c d o)")
 
     with ExitStack() as ctx:
         keep = ctx.enter_context(tc.tile_pool(name="keep", bufs=1))
-        stage = ctx.enter_context(tc.tile_pool(name="stage", bufs=6))
-        small = ctx.enter_context(tc.tile_pool(name="small", bufs=2))
+        stage = ctx.enter_context(tc.tile_pool(name="stage", bufs=5))
+        small = ctx.enter_context(tc.tile_pool(name="small", bufs=4))
         psum = ctx.enter_context(tc.psum_pool(name="psum", bufs=1))
         ctx.enter_context(tc.manual_schedule())
 
         order = []
-        loads = []
-        for g in range(PAIRS):
-            loads.append(("W", 0, g, g + 1))
-            if g == 0:
-                loads.append(("W", 0, 1, 2))
-            elif g + 1 < PAIRS:
-                loads[-1] = ("W", 0, g + 1, g + 2)
-            else:
-                loads.pop()
-            loads.append(("X", 0, g, g + 1))
-            loads.append(("X", 1, g, g + 1))
-        for r in (2, 3):
-            loads.extend([("X", r, 0, 3), ("X", r, 3, 6), ("X", r, 6, 8), ("X", r, 8, 9)])
-        order.append(("A", 0, 0))
-        for g in range(PAIRS):
-            if g + 1 < PAIRS:
-                order.append(("A", 0, g + 1))
-            order.append(("X", 0, g))
-            order.append(("W", 0, g))
-            order.append(("X", 1, g))
-        n_first = len(order)
-        for r in (2, 3):
-            for g in range(PAIRS):
-                order.append(("X", r, g))
-
         groups = []
-        for g in range(PAIRS):
-            groups.append([("W", 0, g)])
-            groups.append([("X", 0, g), ("X", 1, g)])
-        for r in (2, 3):
-            for g in range(0, PAIRS - 1, 2):
-                groups.append([("X", r, g), ("X", r, g + 1)])
-            groups.append([("X", r, PAIRS - 1)])
+        loads = []
+        loads = [("W", [0], p, p + 2) for p in range(0, 18, 2)] + [("X", [0], 0, 4)] + [("W", [0], p, p + 2) for p in range(18, PASSES, 2)]
+        for r in range(B_TILES):
+            cuts = [0, 4, 10, 18] if r == 0 else ([0, 8, 18] if r < 3 else [0, 8, 14, 17, 18])
+            for i in range(len(cuts) - 1):
+                if (r, cuts[i]) not in [(l[1][0], l[2]) for l in loads if l[0] == "X"]:
+                    loads.append(("X", [r], cuts[i], cuts[i + 1]))
+        xs = [("X", r, p, 2) for r in range(B_TILES) for p in range(0, PASSES, 2)]
+        xs = xs[:-1] + [("X", 3, 16, 1), ("X", 3, 17, 1)]
+
+        for p in range(0, 18, 2):
+            order.append(("A", 0, p, 2))
+        n_x = 0
+        for p in range(0, PASSES, 2):
+            order.append(("W", 0, p, 2))
+            if p >= 2:
+                order.extend(xs[n_x : n_x + 1])
+                n_x += 1
+            if p + 18 < PASSES:
+                order.append(("A", 0, p + 18, 2))
+        order.extend(xs[n_x:])
+        ws = [u for u in order if u[0] == "W"]
+        xs = [u for u in order if u[0] == "X"]
+        for i in range(0, len(ws), 1):
+            groups.append(ws[i : i + 1])
+        i = 0
+        while i < len(xs):
+            n = 2 if xs[i : i + 2] and sum(u[3] for u in xs[i : i + 2]) in (1, 2, 4, 8) and i < len(xs) - 2 else 1
+            groups.append(xs[i : i + n])
+            i += n
+
+        x_units = [u for u in order if u[0] == "X"]
+        n_units = len(order)
+        pos = {}
+        for i, unit in enumerate(order):
+            pos[unit] = i
+
+        def on_vector(unit):
+            kind, r, p, n = unit
+            i = pos[unit]
+            if kind == "A":
+                return p % 6 == 2
+            if kind == "W":
+                return p % 4 == 2
+            return (r * PAIRS + p // 2) % 6 == 2
+
 
         def q_lag(members):
-            return 0 if members[0] == ("X", 3, PAIRS - 1) else 1
-
-        mx_at = {}
-        for g in range(1, PAIRS, 2):
-            mx_at[4 * g + 4 + 5] = [(0, g - 1), (1, g - 1), (0, g), (1, g)]
-        mx_at[n_first + 5] = [(0, 8), (1, 8)]
-        mx_at[n_first + 11] = [(2, g) for g in range(6)]
-        sq_at = {n_first + 7: [0], n_first + 9: [1]}
-
+            return 0 if pos[members[-1]] >= n_units - 1 else 1
 
         w_words = {}
         x_words = {}
-        for load in loads:
-            kind, r, g0, g1 = load
-            t = keep.tile([P, (g1 - g0) * 1024], BF16, name="ld%s%d_%d" % (kind, r, g0))
+        for kind, tiles, p0, p1 in loads:
+            n_t = len(tiles)
+            t = keep.tile([P, n_t * (p1 - p0) * 512], BF16, name="ld%s%d_%d" % (kind, tiles[0], p0))
             words = t[:].bitcast(F32)
             if kind == "W":
-                nc.sync.dma_start(out=t[:].rearrange("q (g f) -> q g f", f=1024), in_=w_rows[:, g0:g1, :])
+                nc.sync.dma_start(
+                    out=t[:].rearrange("q (g f) -> q g f", f=1024), in_=w_rows[:, p0 // 2 : p1 // 2, :]
+                )
+            elif n_t == 1:
+                nc.sync.dma_start(out=t[:], in_=x_rows[:, tiles[0], p0 * 512 : p1 * 512])
             else:
-                nc.sync.dma_start(out=t[:], in_=x_rows[r * P : (r + 1) * P, g0 * 1024 : g1 * 1024])
-            for g in range(g0, g1):
-                piece = words[:, (g - g0) * 512 : (g - g0 + 1) * 512]
-                if kind == "W":
-                    w_words[g] = piece.rearrange("q (n e) -> q n e", e=4)
-                else:
-                    x_words[(r, g)] = piece
+                nc.sync.dma_start(
+                    out=t[:].rearrange("q (r k) -> q r k", r=n_t),
+                    in_=x_rows[:, tiles[0] : tiles[0] + n_t, p0 * 512 : p1 * 512],
+                )
+            for i in range(n_t):
+                for p in range(p0, p1):
+                    w0 = (i * (p1 - p0) + p - p0) * 256
+                    if kind == "W":
+                        if p % 2 == 0:
+                            w_words[p] = words[:, w0 : w0 + 512].rearrange("q (n e) -> q n e", e=4)
+                    else:
+                        x_words[(tiles[i], p)] = words[:, w0 : w0 + 256]
 
+        idle = keep.tile([P, 512], BF16, name="idle")
+        nc.vector.memset(idle[:], 1.0)
         warm = keep.tile([P, 2], F32, name="warm")
         nc.vector.memset(warm[:], 1.0)
         nc.scalar.activation(out=warm[:, 1:2], in_=warm[:, 0:1], func=ACTF.Abs_reciprocal_sqrt)
@@ -115,74 +129,93 @@ def tile_digitcaps_kernel(tc, x, W, out):
         make_identity(nc, ident[:])
 
         group_of = {}
-        for members in groups:
-            codes = keep.tile([P, 256 * len(members)], U32, name="c%s%d_%d" % members[0], align_bytes=64)
-            plane = keep.tile([P, 256 * len(members)], U8, name="p%s%d_%d" % members[0], align_bytes=64)
-            entry = [members, codes, plane, None]
-            for unit in members:
-                group_of[unit] = entry
-
-        def operand(unit, half):
-            entry = group_of[unit]
-            c0 = (2 * entry[0].index(unit) + half) * P
-            return entry[1][:, c0 : c0 + P].bitcast(FP8X4), entry[2][:, c0 : c0 + P]
-
-        pos = {}
-        for i, unit in enumerate(order):
-            pos[unit] = i
         q_at = {}
+        q_step = {}
         for members in groups:
+            n_p = sum(u[3] for u in members)
+            name = "%s%d_%d" % (members[0][0], members[0][1], members[0][2])
+            codes = keep.tile([P, P * n_p], U32, name="c" + name, align_bytes=64)
+            plane = keep.tile([P, P * n_p], U8, name="p" + name, align_bytes=64)
             step = max(pos[u] for u in members) + 1 + q_lag(members)
-            q_at.setdefault(step, []).append(members)
+            entry = [members, codes, plane, None, n_p]
+            q_at.setdefault(step, []).append(entry)
+            off = 0
+            for u in members:
+                group_of[u] = (entry, off)
+                for j in range(u[3]):
+                    q_step[(u[0], u[1], u[2] + j)] = (step, entry, off + j)
+                off += u[3]
+
+        def operand(kind, r, p):
+            step, entry, j = q_step[(kind, r, p)]
+            return entry[1][:, j * P : (j + 1) * P].bitcast(FP8X4), entry[2][:, j * P : (j + 1) * P]
+
+        passes = []
+        for u in x_units:
+            for j in range(u[3]):
+                passes.append((u[1], u[2] + j))
+        ready = {}
+        for r, p in passes:
+            ready[(r, p)] = max(q_step[("X", r, p)][0], q_step[("W", 0, p)][0]) + LAG
+        mx_at = {}
+        sq_at = {}
+        done = 0
+        for step in range(n_units - HOLD):
+            n = 0
+            while done + n < len(passes) and n < RUN_MAX and ready[passes[done + n]] <= step:
+                n += 1
+            if n >= (4 if len(mx_at) < 3 else RUN) or (n and passes[done + n - 1][1] == PASSES - 1 and False):
+                mx_at[step] = passes[done : done + n]
+                for r, p in mx_at[step]:
+                    if p == PASSES - 1:
+                        sq_at.setdefault(step + 2, []).append(r)
+                done += n
+        rest = passes[done:]
 
         acc = {}
         sq = {}
         s_tiles = {}
 
         def transposes(unit, ps):
-            kind, r, g = unit
-            for i in range(4):
+            kind, r, p, n = unit
+            for i in range(2 * n):
                 if kind == "A":
-                    src = w_words[g][:, :, i]
+                    src = w_words[p][:, :, i]
                 elif kind == "W":
-                    src = s_tiles[g][:, i * P : (i + 1) * P]
+                    src = s_tiles[p][:, i * P : (i + 1) * P]
                 else:
-                    src = x_words[(r, g)][:, i * P : (i + 1) * P]
+                    src = x_words[(r, p + i // 2)][:, (i % 2) * P : (i % 2 + 1) * P]
                 nc.tensor.transpose(out=ps[:, i * P : (i + 1) * P], in_=src, identity=ident[:])
 
         def evacuate(unit, ps):
-            kind, r, g = unit
+            kind, r, p, n = unit
             if kind == "A":
-                s_tiles[g] = keep.tile([P, 512], F32, name="s%d" % g)
-                dst = s_tiles[g][:].rearrange("n (p e) -> n p e", e=4)
+                s_tiles[p] = keep.tile([P, 512], F32, name="s%d" % p)
+                dst = s_tiles[p][:].rearrange("n (p e) -> n p e", e=4)
                 src = ps[:].rearrange("n (e p) -> n p e", e=4)
             else:
-                entry = group_of[unit]
-                members = entry[0]
+                entry, off = group_of[unit]
                 if entry[3] is None:
-                    tag = "grp%d" % len(members)
-                    entry[3] = stage.tile([P, 1024 * len(members)], BF16, name=tag, tag=tag, align_bytes=64)
-                off = members.index(unit) * 512
-                dst = entry[3][:].bitcast(F32)[:, off : off + 512].rearrange("q (c b u) -> q c b u", c=2, u=2)
-                src = ps[:].rearrange("q (c u b) -> q c b u", c=2, u=2)
+                    tag = "grp%d" % entry[4]
+                    entry[3] = stage.tile([P, 512 * entry[4]], BF16, name=tag, tag=tag, align_bytes=64)
+                dst = entry[3][:].bitcast(F32)[:, off * 256 : (off + n) * 256].rearrange(
+                    "q (c b u) -> q c b u", c=n, u=2
+                )
+                src = ps[:, 0 : n * 256].rearrange("q (c u b) -> q c b u", c=n, u=2)
             if on_vector(unit):
                 nc.vector.tensor_copy(out=dst, in_=src)
             else:
                 nc.scalar.copy(out=dst, in_=src)
 
-        def quantize(members):
-            entry = group_of[members[0]]
-            nc.vector.quantize_mx(out=entry[1][:].bitcast(FP8X4), scales=entry[2][:], in_=entry[3][:])
-
-        def run_mx(r, g):
-            if g == 0:
-                acc[r] = psum.tile([P, N], F32, name="acc%d" % (r % 2), tag="acc%d" % (r % 2))
-            for half in range(2):
-                xc, xp = operand(("X", r, g), half)
-                wc, wp = operand(("W", 0, g), half)
+        def run_mx(run):
+            for r, p in run:
+                if p == 0:
+                    acc[r] = psum.tile([P, N], F32, name="acc%d" % (r % 2), tag="acc%d" % (r % 2))
+                xc, xp = operand("X", r, p)
+                wc, wp = operand("W", 0, p)
                 nc.tensor.matmul_mx(
                     out=acc[r][:], lhsT=xc, lhsT_scale=xp, rhs=wc, rhs_scale=wp,
-                    start=(g == 0 and half == 0), stop=(g == PAIRS - 1 and half == 1),
+                    start=(p == 0), stop=(p == PASSES - 1),
                 )
 
         def squash_a(r):
@@ -210,31 +243,32 @@ def tile_digitcaps_kernel(tc, x, W, out):
             nc.sync.dma_start(out=out_rows[r * P : (r + 1) * P, :], in_=v[:])
 
         banks = {}
-        n_units = len(order)
-        for step in range(n_units + 3):
+        squashed = []
+        for step in range(n_units + 1):
             if step < n_units:
                 ps = psum.tile([P, 512], F32, name="tp%d" % (step % BANKS), tag="tp%d" % (step % BANKS))
                 banks[step] = ps
+                for n in IDLE.get(step, []):
+                    nc.tensor.matmul(out=ps[:, 0:n], lhsT=idle[:, 0:P], rhs=idle[:, 0:n], start=True, stop=True)
                 transposes(order[step], ps)
-            for r, g in mx_at.get(step, []):
-                run_mx(r, g)
-            if 1 <= step <= n_units:
+            if step in mx_at:
+                run_mx(mx_at[step])
+            if step >= 1:
                 evacuate(order[step - 1], banks[step - 1])
-            for members in q_at.get(step, []):
-                quantize(members)
+            for entry in q_at.get(step, []):
+                nc.vector.quantize_mx(out=entry[1][:].bitcast(FP8X4), scales=entry[2][:], in_=entry[3][:])
             for r in sq_at.get(step, []):
                 squash_a(r)
+                squashed.append(r)
             for r in sq_at.get(step - 1, []):
                 squash_b(r)
             for r in sq_at.get(step - 2, []):
                 squash_c(r)
-        for g in range(6, PAIRS):
-            run_mx(2, g)
-        for g in range(0, PAIRS):
-            run_mx(3, g)
-        squash_a(2)
-        squash_b(2)
-        squash_c(2)
-        squash_a(3)
-        squash_b(3)
-        squash_c(3)
+        for r in range(B_TILES):
+            run_mx([rp for rp in rest if rp[0] == r])
+            if r not in squashed:
+                squash_a(r)
+            if r not in squashed or n_units - 1 < max(s for s in sq_at if r in sq_at[s]) + 1 - 1:
+                squash_b(r)
+            if r not in squashed or n_units - 1 < max(s for s in sq_at if r in sq_at[s]) + 2 - 1:
+                squash_c(r)

@@ -22,11 +22,11 @@ FLOPS = 2 * BS * K * N
 BANKS = 6
 C_INV = 1.0 / 1152.0
 
-RUN = 6
+RUN = 10
 RUN_MAX = 10
-LAG = 5
+LAG = 4
 HOLD = 4
-IDLE = {9: [512,512,512], 14: [512], 18: [512]}
+IDLE = {14: [512,512], 17: [512]}
 
 
 def tile_digitcaps_kernel(tc, x, W, out):
@@ -45,25 +45,25 @@ def tile_digitcaps_kernel(tc, x, W, out):
         order = []
         groups = []
         loads = []
-        loads = [("W", [0], p, p + 2) for p in range(0, 18, 2)] + [("X", [0], 0, 4)] + [("W", [0], p, p + 2) for p in range(18, PASSES, 2)]
+        loads = [("W", [0], p, p + 2) for p in range(0, 16, 2)] + [("X", [0], 0, 4)] + [("W", [0], p, p + 2) for p in range(16, PASSES, 2)]
         for r in range(B_TILES):
-            cuts = [0, 4, 10, 18] if r == 0 else ([0, 8, 18] if r < 3 else [0, 8, 14, 17, 18])
+            cuts = [0, 4, 8, 12, 18] if r == 0 else ([0, 6, 12, 18] if r < 3 else [0, 6, 12, 16, 17, 18])
             for i in range(len(cuts) - 1):
                 if (r, cuts[i]) not in [(l[1][0], l[2]) for l in loads if l[0] == "X"]:
                     loads.append(("X", [r], cuts[i], cuts[i + 1]))
         xs = [("X", r, p, 2) for r in range(B_TILES) for p in range(0, PASSES, 2)]
         xs = xs[:-1] + [("X", 3, 16, 1), ("X", 3, 17, 1)]
 
-        for p in range(0, 18, 2):
+        for p in range(0, 8, 2):
             order.append(("A", 0, p, 2))
         n_x = 0
         for p in range(0, PASSES, 2):
             order.append(("W", 0, p, 2))
-            if p >= 2:
-                order.extend(xs[n_x : n_x + 1])
-                n_x += 1
-            if p + 18 < PASSES:
-                order.append(("A", 0, p + 18, 2))
+            if p >= 10:
+                order.extend(xs[n_x : n_x + 3])
+                n_x += 3
+            if p + 8 < PASSES:
+                order.append(("A", 0, p + 8, 2))
         order.extend(xs[n_x:])
         ws = [u for u in order if u[0] == "W"]
         xs = [u for u in order if u[0] == "X"]
@@ -87,8 +87,8 @@ def tile_digitcaps_kernel(tc, x, W, out):
             if kind == "A":
                 return p % 6 == 2
             if kind == "W":
-                return p % 4 == 2
-            return (r * PAIRS + p // 2) % 6 == 2
+                return p % 6 == 2
+            return (r * PAIRS + p // 2) % 5 == 2
 
 
         def q_lag(members):
@@ -164,7 +164,7 @@ def tile_digitcaps_kernel(tc, x, W, out):
             n = 0
             while done + n < len(passes) and n < RUN_MAX and ready[passes[done + n]] <= step:
                 n += 1
-            if n >= (4 if len(mx_at) < 3 else RUN) or (n and passes[done + n - 1][1] == PASSES - 1 and False):
+            if n >= (6 if len(mx_at) < 1 else RUN) or (n and passes[done + n - 1][1] == PASSES - 1 and False):
                 mx_at[step] = passes[done : done + n]
                 for r, p in mx_at[step]:
                     if p == PASSES - 1:

@@ -22,11 +22,11 @@ FLOPS = 2 * BS * K * N
 BANKS = 6
 C_INV = 1.0 / 1152.0
 
-RUN = 10
-RUN_MAX = 10
-LAG = 4
-HOLD = 4
-IDLE = {14: [512,512], 17: [512]}
+RUN = 8
+RUN_MAX = 12
+LAG = 3
+HOLD = 6
+IDLE = {}
 
 
 def tile_digitcaps_kernel(tc, x, W, out):
@@ -45,35 +45,34 @@ def tile_digitcaps_kernel(tc, x, W, out):
         order = []
         groups = []
         loads = []
-        loads = [("W", [0], p, p + 2) for p in range(0, 16, 2)] + [("X", [0], 0, 4)] + [("W", [0], p, p + 2) for p in range(16, PASSES, 2)]
+        w_cuts = [0,2,4,6,10,14,18]
+        loads = [("W", [0], w_cuts[i], w_cuts[i + 1]) for i in range(len(w_cuts) - 1)]
         for r in range(B_TILES):
-            cuts = [0, 4, 8, 12, 18] if r == 0 else ([0, 6, 12, 18] if r < 3 else [0, 6, 12, 16, 17, 18])
+            cuts = [0, 6, 12, 18] if r < 3 else [0, 6, 12, 16, 18]
             for i in range(len(cuts) - 1):
-                if (r, cuts[i]) not in [(l[1][0], l[2]) for l in loads if l[0] == "X"]:
+                if r == 0 and i == 0:
+                    loads.insert(5, ("X", [0], cuts[0], cuts[1]))
+                else:
                     loads.append(("X", [r], cuts[i], cuts[i + 1]))
         xs = [("X", r, p, 2) for r in range(B_TILES) for p in range(0, PASSES, 2)]
         xs = xs[:-1] + [("X", 3, 16, 1), ("X", 3, 17, 1)]
-
-        for p in range(0, 8, 2):
+        for p in range(0, 6, 2):
             order.append(("A", 0, p, 2))
         n_x = 0
         for p in range(0, PASSES, 2):
             order.append(("W", 0, p, 2))
-            if p >= 10:
+            if p >= 8:
                 order.extend(xs[n_x : n_x + 3])
                 n_x += 3
-            if p + 8 < PASSES:
-                order.append(("A", 0, p + 8, 2))
+            if p + 6 < PASSES:
+                order.append(("A", 0, p + 6, 2))
         order.extend(xs[n_x:])
         ws = [u for u in order if u[0] == "W"]
-        xs = [u for u in order if u[0] == "X"]
         for i in range(0, len(ws), 1):
             groups.append(ws[i : i + 1])
-        i = 0
-        while i < len(xs):
-            n = 2 if xs[i : i + 2] and sum(u[3] for u in xs[i : i + 2]) in (1, 2, 4, 8) and i < len(xs) - 2 else 1
-            groups.append(xs[i : i + n])
-            i += n
+        for i in range(0, len(xs) - 3, 2):
+            groups.append(xs[i : i + 2])
+        groups.extend([xs[-3:-2], xs[-2:-1], xs[-1:]])
 
         x_units = [u for u in order if u[0] == "X"]
         n_units = len(order)
@@ -85,10 +84,10 @@ def tile_digitcaps_kernel(tc, x, W, out):
             kind, r, p, n = unit
             i = pos[unit]
             if kind == "A":
-                return p % 6 == 2
+                return False
             if kind == "W":
                 return p % 6 == 2
-            return (r * PAIRS + p // 2) % 5 == 2
+            return (r * 9 + p // 2) % 4 == 2 and r * 9 + p // 2 < 33
 
 
         def q_lag(members):
@@ -120,8 +119,6 @@ def tile_digitcaps_kernel(tc, x, W, out):
                     else:
                         x_words[(tiles[i], p)] = words[:, w0 : w0 + 256]
 
-        idle = keep.tile([P, 512], BF16, name="idle")
-        nc.vector.memset(idle[:], 1.0)
         warm = keep.tile([P, 2], F32, name="warm")
         nc.vector.memset(warm[:], 1.0)
         nc.scalar.activation(out=warm[:, 1:2], in_=warm[:, 0:1], func=ACTF.Abs_reciprocal_sqrt)
@@ -156,19 +153,20 @@ def tile_digitcaps_kernel(tc, x, W, out):
                 passes.append((u[1], u[2] + j))
         ready = {}
         for r, p in passes:
-            ready[(r, p)] = max(q_step[("X", r, p)][0], q_step[("W", 0, p)][0]) + LAG
+            ready[(r, p)] = max(q_step[("X", r, p)][0], q_step[("W", 0, p)][0]) + (2 if r == B_TILES - 1 else LAG)
         mx_at = {}
         sq_at = {}
         done = 0
         for step in range(n_units - HOLD):
             n = 0
-            while done + n < len(passes) and n < RUN_MAX and ready[passes[done + n]] <= step:
+            while done + n < len(passes) and n < (max(RUN_MAX, 6) if len(mx_at) < 2 else RUN_MAX) and ready[passes[done + n]] <= step:
                 n += 1
-            if n >= (6 if len(mx_at) < 1 else RUN) or (n and passes[done + n - 1][1] == PASSES - 1 and False):
+            last = done + n > 0 and passes[done + n - 1][0] == B_TILES - 1
+            if n >= (2 if last else (6 if len(mx_at) < 2 else RUN)):
                 mx_at[step] = passes[done : done + n]
                 for r, p in mx_at[step]:
                     if p == PASSES - 1:
-                        sq_at.setdefault(step + 2, []).append(r)
+                        sq_at.setdefault(step + 3, []).append(r)
                 done += n
         rest = passes[done:]
 
@@ -218,38 +216,51 @@ def tile_digitcaps_kernel(tc, x, W, out):
                     start=(p == 0), stop=(p == PASSES - 1),
                 )
 
-        def squash_a(r):
-            q = small.tile([P, N], F32, name="q")
-            rs = small.tile([P, N], F32, name="rs")
-            nc.scalar.activation(out=q[:], in_=acc[r][:], func=ACTF.Square, scale=C_INV)
-            nc.scalar.activation(out=rs[:], in_=q[:], func=ACTF.Abs_reciprocal_sqrt, bias=1.0)
-            sq[r] = [rs]
+        def squash_a(r, c0, n):
+            q = small.tile([P, n], F32, name="q%d" % n)
+            nc.scalar.activation(out=q[:], in_=acc[r][:, c0 : c0 + n], func=ACTF.Square, scale=C_INV)
+            sq[(r, c0)] = [q]
 
-        def squash_b(r):
-            z = small.tile([P, N], F32, name="z")
+        def squash_b(r, c0, n):
+            rs = small.tile([P, n], F32, name="rs%d" % n)
+            nc.scalar.activation(out=rs[:], in_=sq[(r, c0)][0][:], func=ACTF.Abs_reciprocal_sqrt, bias=1.0)
+            sq[(r, c0)].append(rs)
+
+        def squash_c(r, c0, n):
+            z = small.tile([P, n], F32, name="z%d" % n)
             nc.vector.scalar_tensor_tensor(
-                out=z[:], in0=acc[r][:], scalar=C_INV, in1=sq[r][0][:], op0=ALU.mult, op1=ALU.mult
+                out=z[:], in0=acc[r][:, c0 : c0 + n], scalar=C_INV, in1=sq[(r, c0)][1][:], op0=ALU.mult, op1=ALU.mult
             )
-            sq[r].append(z)
+            sq[(r, c0)].append(z)
 
-        def squash_c(r):
-            z = sq[r][1]
-            az = small.tile([P, N], F32, name="az")
-            v = small.tile([P, N], F32, name="v")
-            nc.vector.scalar_tensor_tensor(
-                out=az[:], in0=z[:], scalar=-1.0, in1=z[:], op0=ALU.mult, op1=ALU.max
-            )
-            nc.vector.tensor_tensor(out=v[:], in0=az[:], in1=z[:], op=ALU.mult)
-            nc.sync.dma_start(out=out_rows[r * P : (r + 1) * P, :], in_=v[:])
+        def squash_d(r, c0, n):
+            az = small.tile([P, n], F32, name="az%d" % n)
+            z = sq[(r, c0)][2]
+            if r < B_TILES - 1:
+                nc.scalar.activation(out=az[:], in_=z[:], func=ACTF.Abs)
+            else:
+                nc.vector.scalar_tensor_tensor(
+                    out=az[:], in0=z[:], scalar=-1.0, in1=z[:], op0=ALU.mult, op1=ALU.max
+                )
+            sq[(r, c0)].append(az)
 
+        def squash_e(r, c0, n):
+            z, az = sq[(r, c0)][2:]
+            if r not in rows:
+                rows[r] = small.tile([P, N], F32, name="rows")
+            engine = nc.gpsimd if r < B_TILES - 1 else nc.vector
+            engine.tensor_tensor(out=rows[r][:, c0 : c0 + n], in0=az[:], in1=z[:], op=ALU.mult)
+
+        def store(r):
+            nc.sync.dma_start(out=out_rows[r * P : (r + 1) * P, :], in_=rows[r][:])
+
+        rows = {}
+        parts = [squash_a, squash_b, squash_c, squash_d, squash_e]
         banks = {}
-        squashed = []
         for step in range(n_units + 1):
             if step < n_units:
                 ps = psum.tile([P, 512], F32, name="tp%d" % (step % BANKS), tag="tp%d" % (step % BANKS))
                 banks[step] = ps
-                for n in IDLE.get(step, []):
-                    nc.tensor.matmul(out=ps[:, 0:n], lhsT=idle[:, 0:P], rhs=idle[:, 0:n], start=True, stop=True)
                 transposes(order[step], ps)
             if step in mx_at:
                 run_mx(mx_at[step])
@@ -257,18 +268,30 @@ def tile_digitcaps_kernel(tc, x, W, out):
                 evacuate(order[step - 1], banks[step - 1])
             for entry in q_at.get(step, []):
                 nc.vector.quantize_mx(out=entry[1][:].bitcast(FP8X4), scales=entry[2][:], in_=entry[3][:])
-            for r in sq_at.get(step, []):
-                squash_a(r)
-                squashed.append(r)
-            for r in sq_at.get(step - 1, []):
-                squash_b(r)
-            for r in sq_at.get(step - 2, []):
-                squash_c(r)
-        for r in range(B_TILES):
+            for lag in range(5):
+                for r in sq_at.get(step - lag, []):
+                    parts[lag](r, 0, N)
+                    if lag == 4:
+                        store(r)
+        begun = {}
+        for step in sq_at:
+            for r in sq_at[step]:
+                begun[r] = step
+        last = B_TILES - 1
+
+        def finish(r, lags):
+            begin = begun.get(r, n_units + 1)
+            for lag in lags:
+                if begin + lag > n_units:
+                    parts[lag](r, 0, N)
+                    if lag == 4:
+                        store(r)
+
+        for r in range(last):
             run_mx([rp for rp in rest if rp[0] == r])
-            if r not in squashed:
-                squash_a(r)
-            if r not in squashed or n_units - 1 < max(s for s in sq_at if r in sq_at[s]) + 1 - 1:
-                squash_b(r)
-            if r not in squashed or n_units - 1 < max(s for s in sq_at if r in sq_at[s]) + 2 - 1:
-                squash_c(r)
+            finish(r, (0, 1, 2))
+        run_mx([rp for rp in rest if rp[0] == last])
+        finish(last, (0, 1))
+        for r in range(last):
+            finish(r, (3, 4))
+        finish(last, (2, 3, 4))

@@ -13,20 +13,25 @@ ALU = mybir.AluOpType
 
 P = 128
 BS = 512
-K = 9216
+CAPSULES = 1152
+K = CAPSULES * 8
 N = 128
+TILES = BS // P
 PASSES = K // 512
-PAIRS = PASSES // 2
-B_TILES = BS // P
 FLOPS = 2 * BS * K * N
-BANKS = 6
-C_INV = 1.0 / 1152.0
 
+WORDS = 256
+BANKS = 6
+AHEAD = 3
+WOVEN_FROM = 4
+WOVEN = 2
 RUN = 8
-RUN_MAX = 12
 LAG = 3
-HOLD = 6
-IDLE = {}
+SUM_LAG = 3
+
+W_CUTS = (0, 2, 4, 6, 10, 14, 18)
+X_CUTS = (0, 6, 12, 18)
+X_CUTS_LAST = (0, 6, 12, 16, 18)
 
 
 def tile_digitcaps_kernel(tc, x, W, out):
@@ -35,6 +40,37 @@ def tile_digitcaps_kernel(tc, x, W, out):
     w_rows = W.rearrange("o (g q) c d e -> q (o g) (c d e)", q=P)
     out_rows = out.rearrange("b c d o -> b (c d o)")
 
+    x_units = [("X", r, p, 2) for r in range(TILES) for p in range(0, PASSES, 2)]
+    x_units[-1:] = [("X", TILES - 1, PASSES - 2, 1), ("X", TILES - 1, PASSES - 1, 1)]
+    w1_units = [("W1", 0, p, 2) for p in range(0, PASSES, 2)]
+    w2_units = [("W2", 0, p, 2) for p in range(0, PASSES, 2)]
+    order = w1_units[:AHEAD]
+    woven = 0
+    for i in range(len(w2_units)):
+        order.append(w2_units[i])
+        if i >= WOVEN_FROM:
+            order.extend(x_units[woven : woven + WOVEN])
+            woven += WOVEN
+        order.extend(w1_units[i + AHEAD : i + AHEAD + 1])
+    order.extend(x_units[woven:])
+    n_units = len(order)
+    place = {}
+    for i, unit in enumerate(order):
+        place[unit] = i
+
+    groups = [[u] for u in w2_units]
+    groups.extend([x_units[i : i + 2] for i in range(0, len(x_units) - 3, 2)])
+    groups.extend([[u] for u in x_units[-3:]])
+
+    def on_vector(unit):
+        kind, r, p, n = unit
+        if kind == "W1":
+            return False
+        if kind == "W2":
+            return p // 2 % 3 == 1
+        i = r * (PASSES // 2) + p // 2
+        return i % 4 == 2 and i < TILES * (PASSES // 2) - 3
+
     with ExitStack() as ctx:
         keep = ctx.enter_context(tc.tile_pool(name="keep", bufs=1))
         stage = ctx.enter_context(tc.tile_pool(name="stage", bufs=5))
@@ -42,256 +78,188 @@ def tile_digitcaps_kernel(tc, x, W, out):
         psum = ctx.enter_context(tc.psum_pool(name="psum", bufs=1))
         ctx.enter_context(tc.manual_schedule())
 
-        order = []
-        groups = []
-        loads = []
-        w_cuts = [0,2,4,6,10,14,18]
-        loads = [("W", [0], w_cuts[i], w_cuts[i + 1]) for i in range(len(w_cuts) - 1)]
-        for r in range(B_TILES):
-            cuts = [0, 6, 12, 18] if r < 3 else [0, 6, 12, 16, 18]
-            for i in range(len(cuts) - 1):
-                if r == 0 and i == 0:
-                    loads.insert(5, ("X", [0], cuts[0], cuts[1]))
-                else:
-                    loads.append(("X", [r], cuts[i], cuts[i + 1]))
-        xs = [("X", r, p, 2) for r in range(B_TILES) for p in range(0, PASSES, 2)]
-        xs = xs[:-1] + [("X", 3, 16, 1), ("X", 3, 17, 1)]
-        for p in range(0, 6, 2):
-            order.append(("A", 0, p, 2))
-        n_x = 0
-        for p in range(0, PASSES, 2):
-            order.append(("W", 0, p, 2))
-            if p >= 8:
-                order.extend(xs[n_x : n_x + 3])
-                n_x += 3
-            if p + 6 < PASSES:
-                order.append(("A", 0, p + 6, 2))
-        order.extend(xs[n_x:])
-        ws = [u for u in order if u[0] == "W"]
-        for i in range(0, len(ws), 1):
-            groups.append(ws[i : i + 1])
-        for i in range(0, len(xs) - 3, 2):
-            groups.append(xs[i : i + 2])
-        groups.extend([xs[-3:-2], xs[-2:-1], xs[-1:]])
-
-        x_units = [u for u in order if u[0] == "X"]
-        n_units = len(order)
-        pos = {}
-        for i, unit in enumerate(order):
-            pos[unit] = i
-
-        def on_vector(unit):
-            kind, r, p, n = unit
-            i = pos[unit]
-            if kind == "A":
-                return False
-            if kind == "W":
-                return p % 6 == 2
-            return (r * 9 + p // 2) % 4 == 2 and r * 9 + p // 2 < 33
-
-
-        def q_lag(members):
-            return 0 if pos[members[-1]] >= n_units - 1 else 1
-
+        loads = [("W", 0, W_CUTS[i], W_CUTS[i + 1]) for i in range(len(W_CUTS) - 1)]
+        for r in range(TILES):
+            cuts = X_CUTS_LAST if r == TILES - 1 else X_CUTS
+            loads.extend([("X", r, cuts[i], cuts[i + 1]) for i in range(len(cuts) - 1)])
+        i = len(W_CUTS) - 2
+        loads[i], loads[i + 1] = loads[i + 1], loads[i]
         w_words = {}
         x_words = {}
-        for kind, tiles, p0, p1 in loads:
-            n_t = len(tiles)
-            t = keep.tile([P, n_t * (p1 - p0) * 512], BF16, name="ld%s%d_%d" % (kind, tiles[0], p0))
-            words = t[:].bitcast(F32)
+        for kind, r, p0, p1 in loads:
+            raw = keep.tile([P, (p1 - p0) * 2 * WORDS], BF16, name="raw%s%d_%d" % (kind, r, p0))
+            words = raw[:].bitcast(F32)
             if kind == "W":
                 nc.sync.dma_start(
-                    out=t[:].rearrange("q (g f) -> q g f", f=1024), in_=w_rows[:, p0 // 2 : p1 // 2, :]
+                    out=raw[:].rearrange("q (g f) -> q g f", f=4 * WORDS), in_=w_rows[:, p0 // 2 : p1 // 2, :]
                 )
-            elif n_t == 1:
-                nc.sync.dma_start(out=t[:], in_=x_rows[:, tiles[0], p0 * 512 : p1 * 512])
+                for p in range(p0, p1, 2):
+                    piece = words[:, (p - p0) * WORDS : (p - p0 + 2) * WORDS]
+                    w_words[p] = piece.rearrange("q (n j) -> q n j", n=N)
             else:
-                nc.sync.dma_start(
-                    out=t[:].rearrange("q (r k) -> q r k", r=n_t),
-                    in_=x_rows[:, tiles[0] : tiles[0] + n_t, p0 * 512 : p1 * 512],
-                )
-            for i in range(n_t):
+                nc.sync.dma_start(out=raw[:], in_=x_rows[:, r, p0 * 2 * WORDS : p1 * 2 * WORDS])
                 for p in range(p0, p1):
-                    w0 = (i * (p1 - p0) + p - p0) * 256
-                    if kind == "W":
-                        if p % 2 == 0:
-                            w_words[p] = words[:, w0 : w0 + 512].rearrange("q (n e) -> q n e", e=4)
-                    else:
-                        x_words[(tiles[i], p)] = words[:, w0 : w0 + 256]
+                    x_words[(r, p)] = words[:, (p - p0) * WORDS : (p - p0 + 1) * WORDS]
 
-        warm = keep.tile([P, 2], F32, name="warm")
-        nc.vector.memset(warm[:], 1.0)
-        nc.scalar.activation(out=warm[:, 1:2], in_=warm[:, 0:1], func=ACTF.Abs_reciprocal_sqrt)
+        table = keep.tile([P, 2], F32, name="table")
+        nc.vector.memset(table[:], 1.0)
+        nc.scalar.activation(out=table[:, 1:2], in_=table[:, 0:1], func=ACTF.Abs_reciprocal_sqrt)
         ident = keep.tile([P, P], F32, name="ident")
         make_identity(nc, ident[:])
 
         group_of = {}
-        q_at = {}
-        q_step = {}
-        for members in groups:
+        staged = {}
+        codes = []
+        scales = []
+        quantize_at = {}
+        where = {}
+        quantized = {}
+        for g, members in enumerate(groups):
             n_p = sum(u[3] for u in members)
-            name = "%s%d_%d" % (members[0][0], members[0][1], members[0][2])
-            codes = keep.tile([P, P * n_p], U32, name="c" + name, align_bytes=64)
-            plane = keep.tile([P, P * n_p], U8, name="p" + name, align_bytes=64)
-            step = max(pos[u] for u in members) + 1 + q_lag(members)
-            entry = [members, codes, plane, None, n_p]
-            q_at.setdefault(step, []).append(entry)
-            off = 0
-            for u in members:
-                group_of[u] = (entry, off)
-                for j in range(u[3]):
-                    q_step[(u[0], u[1], u[2] + j)] = (step, entry, off + j)
-                off += u[3]
+            codes.append(keep.tile([P, n_p * P], U32, name="codes%d" % g, align_bytes=64))
+            scales.append(keep.tile([P, n_p * P], U8, name="scales%d" % g, align_bytes=64))
+            i = place[members[-1]]
+            step = i + 1 if i == n_units - 1 else i + 2
+            quantize_at.setdefault(step, []).append(g)
+            before = 0
+            for kind, r, p, n in members:
+                group_of[(kind, r, p, n)] = (g, before)
+                for j in range(n):
+                    where[(kind, r, p + j)] = (g, before + j)
+                    quantized[(kind, r, p + j)] = step
+                before += n
 
         def operand(kind, r, p):
-            step, entry, j = q_step[(kind, r, p)]
-            return entry[1][:, j * P : (j + 1) * P].bitcast(FP8X4), entry[2][:, j * P : (j + 1) * P]
+            g, i = where[(kind, r, p)]
+            return codes[g][:, i * P : (i + 1) * P].bitcast(FP8X4), scales[g][:, i * P : (i + 1) * P]
 
-        passes = []
-        for u in x_units:
-            for j in range(u[3]):
-                passes.append((u[1], u[2] + j))
-        ready = {}
-        for r, p in passes:
-            ready[(r, p)] = max(q_step[("X", r, p)][0], q_step[("W", 0, p)][0]) + (2 if r == B_TILES - 1 else LAG)
-        mx_at = {}
-        sq_at = {}
+        passes = [(r, p) for r in range(TILES) for p in range(PASSES)]
+        run_at = {}
+        squash_at = {}
         done = 0
-        for step in range(n_units - HOLD):
-            n = 0
-            while done + n < len(passes) and n < (max(RUN_MAX, 6) if len(mx_at) < 2 else RUN_MAX) and ready[passes[done + n]] <= step:
-                n += 1
-            last = done + n > 0 and passes[done + n - 1][0] == B_TILES - 1
-            if n >= (2 if last else (6 if len(mx_at) < 2 else RUN)):
-                mx_at[step] = passes[done : done + n]
-                for r, p in mx_at[step]:
+        for step in range(n_units - BANKS):
+            ready = 0
+            for r, p in passes[done : done + RUN]:
+                if max(quantized[("X", r, p)], quantized[("W2", 0, p)]) + LAG > step:
+                    break
+                ready += 1
+            if ready == RUN:
+                run_at[step] = passes[done : done + RUN]
+                done += RUN
+                for r, p in run_at[step]:
                     if p == PASSES - 1:
-                        sq_at.setdefault(step + 3, []).append(r)
-                done += n
-        rest = passes[done:]
+                        squash_at[r] = step + SUM_LAG
 
-        acc = {}
-        sq = {}
-        s_tiles = {}
+        w_turned = {}
+        sums = {}
+        parts = {}
 
-        def transposes(unit, ps):
+        def transposes(unit, bank):
             kind, r, p, n = unit
             for i in range(2 * n):
-                if kind == "A":
+                if kind == "W1":
                     src = w_words[p][:, :, i]
-                elif kind == "W":
-                    src = s_tiles[p][:, i * P : (i + 1) * P]
+                elif kind == "W2":
+                    src = w_turned[p][:, i * P : (i + 1) * P]
                 else:
-                    src = x_words[(r, p + i // 2)][:, (i % 2) * P : (i % 2 + 1) * P]
-                nc.tensor.transpose(out=ps[:, i * P : (i + 1) * P], in_=src, identity=ident[:])
+                    src = x_words[(r, p + i // 2)][:, i % 2 * P : (i % 2 + 1) * P]
+                nc.tensor.transpose(out=bank[:, i * P : (i + 1) * P], in_=src, identity=ident[:])
 
-        def evacuate(unit, ps):
+        def copy_out(unit, bank):
             kind, r, p, n = unit
-            if kind == "A":
-                s_tiles[p] = keep.tile([P, 512], F32, name="s%d" % p)
-                dst = s_tiles[p][:].rearrange("n (p e) -> n p e", e=4)
-                src = ps[:].rearrange("n (e p) -> n p e", e=4)
+            if kind == "W1":
+                w_turned[p] = keep.tile([P, 2 * WORDS], F32, name="turned%d" % p)
+                dst = w_turned[p][:].rearrange("n (p j) -> n p j", j=4)
+                src = bank[:].rearrange("n (j p) -> n p j", j=4)
             else:
-                entry, off = group_of[unit]
-                if entry[3] is None:
-                    tag = "grp%d" % entry[4]
-                    entry[3] = stage.tile([P, 512 * entry[4]], BF16, name=tag, tag=tag, align_bytes=64)
-                dst = entry[3][:].bitcast(F32)[:, off * 256 : (off + n) * 256].rearrange(
-                    "q (c b u) -> q c b u", c=n, u=2
-                )
-                src = ps[:, 0 : n * 256].rearrange("q (c u b) -> q c b u", c=n, u=2)
+                g, before = group_of[unit]
+                if g not in staged:
+                    width = sum(u[3] for u in groups[g]) * 4 * P
+                    staged[g] = stage.tile(
+                        [P, width], BF16, name="staged%d" % width, tag="staged%d" % width, align_bytes=64
+                    )
+                words = staged[g][:].bitcast(F32)[:, before * WORDS : (before + n) * WORDS]
+                dst = words.rearrange("q (i b u) -> q i b u", i=n, u=2)
+                src = bank[:, 0 : n * WORDS].rearrange("q (i u b) -> q i b u", i=n, u=2)
             if on_vector(unit):
                 nc.vector.tensor_copy(out=dst, in_=src)
             else:
                 nc.scalar.copy(out=dst, in_=src)
 
-        def run_mx(run):
+        def multiply(run):
             for r, p in run:
                 if p == 0:
-                    acc[r] = psum.tile([P, N], F32, name="acc%d" % (r % 2), tag="acc%d" % (r % 2))
-                xc, xp = operand("X", r, p)
-                wc, wp = operand("W", 0, p)
+                    sums[r] = psum.tile([P, N], F32, name="sums%d" % (r % 2), tag="sums%d" % (r % 2))
+                x_codes, x_scales = operand("X", r, p)
+                w_codes, w_scales = operand("W2", 0, p)
                 nc.tensor.matmul_mx(
-                    out=acc[r][:], lhsT=xc, lhsT_scale=xp, rhs=wc, rhs_scale=wp,
-                    start=(p == 0), stop=(p == PASSES - 1),
+                    out=sums[r][:],
+                    lhsT=x_codes,
+                    lhsT_scale=x_scales,
+                    rhs=w_codes,
+                    rhs_scale=w_scales,
+                    start=(p == 0),
+                    stop=(p == PASSES - 1),
                 )
 
-        def squash_a(r, c0, n):
-            q = small.tile([P, n], F32, name="q%d" % n)
-            nc.scalar.activation(out=q[:], in_=acc[r][:, c0 : c0 + n], func=ACTF.Square, scale=C_INV)
-            sq[(r, c0)] = [q]
-
-        def squash_b(r, c0, n):
-            rs = small.tile([P, n], F32, name="rs%d" % n)
-            nc.scalar.activation(out=rs[:], in_=sq[(r, c0)][0][:], func=ACTF.Abs_reciprocal_sqrt, bias=1.0)
-            sq[(r, c0)].append(rs)
-
-        def squash_c(r, c0, n):
-            z = small.tile([P, n], F32, name="z%d" % n)
-            nc.vector.scalar_tensor_tensor(
-                out=z[:], in0=acc[r][:, c0 : c0 + n], scalar=C_INV, in1=sq[(r, c0)][1][:], op0=ALU.mult, op1=ALU.mult
-            )
-            sq[(r, c0)].append(z)
-
-        def squash_d(r, c0, n):
-            az = small.tile([P, n], F32, name="az%d" % n)
-            z = sq[(r, c0)][2]
-            if r < B_TILES - 1:
-                nc.scalar.activation(out=az[:], in_=z[:], func=ACTF.Abs)
-            else:
+        def squash(r, i):
+            if i == 0:
+                square = small.tile([P, N], F32, name="square")
+                nc.scalar.activation(out=square[:], in_=sums[r][:], func=ACTF.Square, scale=1.0 / CAPSULES)
+                parts[r] = square
+            elif i == 1:
+                root = small.tile([P, N], F32, name="root")
+                nc.scalar.activation(out=root[:], in_=parts[r][:], func=ACTF.Abs_reciprocal_sqrt, bias=1.0)
+                parts[r] = root
+            elif i == 2:
+                z = small.tile([P, N], F32, name="z")
                 nc.vector.scalar_tensor_tensor(
-                    out=az[:], in0=z[:], scalar=-1.0, in1=z[:], op0=ALU.mult, op1=ALU.max
+                    out=z[:], in0=sums[r][:], scalar=1.0 / CAPSULES, in1=parts[r][:], op0=ALU.mult, op1=ALU.mult
                 )
-            sq[(r, c0)].append(az)
+                parts[r] = z
+            elif i == 3:
+                size = small.tile([P, N], F32, name="size")
+                z = parts[r]
+                if r < TILES - 1:
+                    nc.scalar.activation(out=size[:], in_=z[:], func=ACTF.Abs)
+                else:
+                    nc.vector.scalar_tensor_tensor(
+                        out=size[:], in0=z[:], scalar=-1.0, in1=z[:], op0=ALU.mult, op1=ALU.max
+                    )
+                parts[r] = (z, size)
+            else:
+                z, size = parts[r]
+                result = small.tile([P, N], F32, name="result")
+                engine = nc.gpsimd if r < TILES - 1 else nc.vector
+                engine.tensor_tensor(out=result[:], in0=size[:], in1=z[:], op=ALU.mult)
+                nc.sync.dma_start(out=out_rows[r * P : (r + 1) * P, :], in_=result[:])
 
-        def squash_e(r, c0, n):
-            z, az = sq[(r, c0)][2:]
-            if r not in rows:
-                rows[r] = small.tile([P, N], F32, name="rows")
-            engine = nc.gpsimd if r < B_TILES - 1 else nc.vector
-            engine.tensor_tensor(out=rows[r][:, c0 : c0 + n], in0=az[:], in1=z[:], op=ALU.mult)
-
-        def store(r):
-            nc.sync.dma_start(out=out_rows[r * P : (r + 1) * P, :], in_=rows[r][:])
-
-        rows = {}
-        parts = [squash_a, squash_b, squash_c, squash_d, squash_e]
         banks = {}
         for step in range(n_units + 1):
             if step < n_units:
-                ps = psum.tile([P, 512], F32, name="tp%d" % (step % BANKS), tag="tp%d" % (step % BANKS))
-                banks[step] = ps
-                transposes(order[step], ps)
-            if step in mx_at:
-                run_mx(mx_at[step])
-            if step >= 1:
-                evacuate(order[step - 1], banks[step - 1])
-            for entry in q_at.get(step, []):
-                nc.vector.quantize_mx(out=entry[1][:].bitcast(FP8X4), scales=entry[2][:], in_=entry[3][:])
-            for lag in range(5):
-                for r in sq_at.get(step - lag, []):
-                    parts[lag](r, 0, N)
-                    if lag == 4:
-                        store(r)
-        begun = {}
-        for step in sq_at:
-            for r in sq_at[step]:
-                begun[r] = step
-        last = B_TILES - 1
+                name = "turn%d" % (step % BANKS)
+                banks[step] = psum.tile([P, 2 * WORDS], F32, name=name, tag=name)
+                transposes(order[step], banks[step])
+            multiply(run_at.get(step, []))
+            if step > 0:
+                copy_out(order[step - 1], banks[step - 1])
+            for g in quantize_at.get(step, []):
+                nc.vector.quantize_mx(out=codes[g][:].bitcast(FP8X4), scales=scales[g][:], in_=staged[g][:])
+            for r in squash_at:
+                if 0 <= step - squash_at[r] <= 4:
+                    squash(r, step - squash_at[r])
 
-        def finish(r, lags):
-            begin = begun.get(r, n_units + 1)
-            for lag in lags:
-                if begin + lag > n_units:
-                    parts[lag](r, 0, N)
-                    if lag == 4:
-                        store(r)
+        def finish(r, first, last):
+            for i in range(first, last + 1):
+                if squash_at.get(r, n_units + 1) + i > n_units:
+                    squash(r, i)
 
-        for r in range(last):
-            run_mx([rp for rp in rest if rp[0] == r])
-            finish(r, (0, 1, 2))
-        run_mx([rp for rp in rest if rp[0] == last])
-        finish(last, (0, 1))
-        for r in range(last):
-            finish(r, (3, 4))
-        finish(last, (2, 3, 4))
+        final = TILES - 1
+        for r in range(final):
+            multiply([rp for rp in passes[done:] if rp[0] == r])
+            finish(r, 0, 2)
+        multiply([rp for rp in passes[done:] if rp[0] == final])
+        finish(final, 0, 1)
+        for r in range(final):
+            finish(r, 3, 4)
+        finish(final, 2, 4)

from contextlib import ExitStack

import concourse.mybir as mybir
from concourse.masks import make_identity

F32 = mybir.dt.float32
BF16 = mybir.dt.bfloat16
U32 = mybir.dt.uint32
U8 = mybir.dt.uint8
FP8X4 = mybir.dt.float8_e4m3fn_x4
ACTF = mybir.ActivationFunctionType
ALU = mybir.AluOpType

P = 128
BS = 512
CAPSULES = 1152
K = CAPSULES * 8
N = 128
TILES = BS // P
PASSES = K // 512
FLOPS = 2 * BS * K * N

WORDS = 256
BANKS = 6
AHEAD = 3
WOVEN_FROM = 4
WOVEN = 2
RUN = 8
LAG = 3
SUM_LAG = 3

W_CUTS = (0, 2, 4, 6, 10, 14, 18)
X_CUTS = (0, 6, 12, 18)
X_CUTS_LAST = (0, 6, 12, 16, 18)


def tile_digitcaps_kernel(tc, x, W, out):
    nc = tc.nc
    x_rows = x.rearrange("(r q) p e -> q r (p e)", q=P)
    w_rows = W.rearrange("o (g q) c d e -> q (o g) (c d e)", q=P)
    out_rows = out.rearrange("b c d o -> b (c d o)")

    x_units = [("X", r, p, 2) for r in range(TILES) for p in range(0, PASSES, 2)]
    x_units[-1:] = [("X", TILES - 1, PASSES - 2, 1), ("X", TILES - 1, PASSES - 1, 1)]
    w1_units = [("W1", 0, p, 2) for p in range(0, PASSES, 2)]
    w2_units = [("W2", 0, p, 2) for p in range(0, PASSES, 2)]
    order = w1_units[:AHEAD]
    woven = 0
    for i in range(len(w2_units)):
        order.append(w2_units[i])
        if i >= WOVEN_FROM:
            order.extend(x_units[woven : woven + WOVEN])
            woven += WOVEN
        order.extend(w1_units[i + AHEAD : i + AHEAD + 1])
    order.extend(x_units[woven:])
    n_units = len(order)
    place = {}
    for i, unit in enumerate(order):
        place[unit] = i

    groups = [[u] for u in w2_units]
    groups.extend([x_units[i : i + 2] for i in range(0, len(x_units) - 3, 2)])
    groups.extend([[u] for u in x_units[-3:]])

    def on_vector(unit):
        kind, r, p, n = unit
        if kind == "W1":
            return False
        if kind == "W2":
            return p // 2 % 3 == 1
        i = r * (PASSES // 2) + p // 2
        return i % 4 == 2 and i < TILES * (PASSES // 2) - 3

    with ExitStack() as ctx:
        keep = ctx.enter_context(tc.tile_pool(name="keep", bufs=1))
        stage = ctx.enter_context(tc.tile_pool(name="stage", bufs=5))
        small = ctx.enter_context(tc.tile_pool(name="small", bufs=4))
        psum = ctx.enter_context(tc.psum_pool(name="psum", bufs=1))
        ctx.enter_context(tc.manual_schedule())

        loads = [("W", 0, W_CUTS[i], W_CUTS[i + 1]) for i in range(len(W_CUTS) - 1)]
        for r in range(TILES):
            cuts = X_CUTS_LAST if r == TILES - 1 else X_CUTS
            loads.extend([("X", r, cuts[i], cuts[i + 1]) for i in range(len(cuts) - 1)])
        i = len(W_CUTS) - 2
        loads[i], loads[i + 1] = loads[i + 1], loads[i]
        w_words = {}
        x_words = {}
        for kind, r, p0, p1 in loads:
            raw = keep.tile([P, (p1 - p0) * 2 * WORDS], BF16, name="raw%s%d_%d" % (kind, r, p0))
            words = raw[:].bitcast(F32)
            if kind == "W":
                nc.sync.dma_start(
                    out=raw[:].rearrange("q (g f) -> q g f", f=4 * WORDS), in_=w_rows[:, p0 // 2 : p1 // 2, :]
                )
                for p in range(p0, p1, 2):
                    piece = words[:, (p - p0) * WORDS : (p - p0 + 2) * WORDS]
                    w_words[p] = piece.rearrange("q (n j) -> q n j", n=N)
            else:
                nc.sync.dma_start(out=raw[:], in_=x_rows[:, r, p0 * 2 * WORDS : p1 * 2 * WORDS])
                for p in range(p0, p1):
                    x_words[(r, p)] = words[:, (p - p0) * WORDS : (p - p0 + 1) * WORDS]

        table = keep.tile([P, 2], F32, name="table")
        nc.vector.memset(table[:], 1.0)
        nc.scalar.activation(out=table[:, 1:2], in_=table[:, 0:1], func=ACTF.Abs_reciprocal_sqrt)
        ident = keep.tile([P, P], F32, name="ident")
        make_identity(nc, ident[:])

        group_of = {}
        staged = {}
        codes = []
        scales = []
        quantize_at = {}
        where = {}
        quantized = {}
        for g, members in enumerate(groups):
            n_p = sum(u[3] for u in members)
            codes.append(keep.tile([P, n_p * P], U32, name="codes%d" % g, align_bytes=64))
            scales.append(keep.tile([P, n_p * P], U8, name="scales%d" % g, align_bytes=64))
            i = place[members[-1]]
            step = i + 1 if i == n_units - 1 else i + 2
            quantize_at.setdefault(step, []).append(g)
            before = 0
            for kind, r, p, n in members:
                group_of[(kind, r, p, n)] = (g, before)
                for j in range(n):
                    where[(kind, r, p + j)] = (g, before + j)
                    quantized[(kind, r, p + j)] = step
                before += n

        def operand(kind, r, p):
            g, i = where[(kind, r, p)]
            return codes[g][:, i * P : (i + 1) * P].bitcast(FP8X4), scales[g][:, i * P : (i + 1) * P]

        passes = [(r, p) for r in range(TILES) for p in range(PASSES)]
        run_at = {}
        squash_at = {}
        done = 0
        for step in range(n_units - BANKS):
            ready = 0
            for r, p in passes[done : done + RUN]:
                if max(quantized[("X", r, p)], quantized[("W2", 0, p)]) + LAG > step:
                    break
                ready += 1
            if ready == RUN:
                run_at[step] = passes[done : done + RUN]
                done += RUN
                for r, p in run_at[step]:
                    if p == PASSES - 1:
                        squash_at[r] = step + SUM_LAG

        w_turned = {}
        sums = {}
        parts = {}

        def transposes(unit, bank):
            kind, r, p, n = unit
            for i in range(2 * n):
                if kind == "W1":
                    src = w_words[p][:, :, i]
                elif kind == "W2":
                    src = w_turned[p][:, i * P : (i + 1) * P]
                else:
                    src = x_words[(r, p + i // 2)][:, i % 2 * P : (i % 2 + 1) * P]
                nc.tensor.transpose(out=bank[:, i * P : (i + 1) * P], in_=src, identity=ident[:])

        def copy_out(unit, bank):
            kind, r, p, n = unit
            if kind == "W1":
                w_turned[p] = keep.tile([P, 2 * WORDS], F32, name="turned%d" % p)
                dst = w_turned[p][:].rearrange("n (p j) -> n p j", j=4)
                src = bank[:].rearrange("n (j p) -> n p j", j=4)
            else:
                g, before = group_of[unit]
                if g not in staged:
                    width = sum(u[3] for u in groups[g]) * 4 * P
                    staged[g] = stage.tile(
                        [P, width], BF16, name="staged%d" % width, tag="staged%d" % width, align_bytes=64
                    )
                words = staged[g][:].bitcast(F32)[:, before * WORDS : (before + n) * WORDS]
                dst = words.rearrange("q (i b u) -> q i b u", i=n, u=2)
                src = bank[:, 0 : n * WORDS].rearrange("q (i u b) -> q i b u", i=n, u=2)
            if on_vector(unit):
                nc.vector.tensor_copy(out=dst, in_=src)
            else:
                nc.scalar.copy(out=dst, in_=src)

        def multiply(run):
            for r, p in run:
                if p == 0:
                    sums[r] = psum.tile([P, N], F32, name="sums%d" % (r % 2), tag="sums%d" % (r % 2))
                x_codes, x_scales = operand("X", r, p)
                w_codes, w_scales = operand("W2", 0, p)
                nc.tensor.matmul_mx(
                    out=sums[r][:],
                    lhsT=x_codes,
                    lhsT_scale=x_scales,
                    rhs=w_codes,
                    rhs_scale=w_scales,
                    start=(p == 0),
                    stop=(p == PASSES - 1),
                )

        def squash(r, i):
            if i == 0:
                square = small.tile([P, N], F32, name="square")
                nc.scalar.activation(out=square[:], in_=sums[r][:], func=ACTF.Square, scale=1.0 / CAPSULES)
                parts[r] = square
            elif i == 1:
                root = small.tile([P, N], F32, name="root")
                nc.scalar.activation(out=root[:], in_=parts[r][:], func=ACTF.Abs_reciprocal_sqrt, bias=1.0)
                parts[r] = root
            elif i == 2:
                z = small.tile([P, N], F32, name="z")
                nc.vector.scalar_tensor_tensor(
                    out=z[:], in0=sums[r][:], scalar=1.0 / CAPSULES, in1=parts[r][:], op0=ALU.mult, op1=ALU.mult
                )
                parts[r] = z
            elif i == 3:
                size = small.tile([P, N], F32, name="size")
                z = parts[r]
                if r < TILES - 1:
                    nc.scalar.activation(out=size[:], in_=z[:], func=ACTF.Abs)
                else:
                    nc.vector.scalar_tensor_tensor(
                        out=size[:], in0=z[:], scalar=-1.0, in1=z[:], op0=ALU.mult, op1=ALU.max
                    )
                parts[r] = (z, size)
            else:
                z, size = parts[r]
                result = small.tile([P, N], F32, name="result")
                engine = nc.gpsimd if r < TILES - 1 else nc.vector
                engine.tensor_tensor(out=result[:], in0=size[:], in1=z[:], op=ALU.mult)
                nc.sync.dma_start(out=out_rows[r * P : (r + 1) * P, :], in_=result[:])

        banks = {}
        for step in range(n_units + 1):
            if step < n_units:
                name = "turn%d" % (step % BANKS)
                banks[step] = psum.tile([P, 2 * WORDS], F32, name=name, tag=name)
                transposes(order[step], banks[step])
            multiply(run_at.get(step, []))
            if step > 0:
                copy_out(order[step - 1], banks[step - 1])
            for g in quantize_at.get(step, []):
                nc.vector.quantize_mx(out=codes[g][:].bitcast(FP8X4), scales=scales[g][:], in_=staged[g][:])
            for r in squash_at:
                if 0 <= step - squash_at[r] <= 4:
                    squash(r, step - squash_at[r])

        def finish(r, first, last):
            for i in range(first, last + 1):
                if squash_at.get(r, n_units + 1) + i > n_units:
                    squash(r, i)

        final = TILES - 1
        for r in range(final):
            multiply([rp for rp in passes[done:] if rp[0] == r])
            finish(r, 0, 2)
        multiply([rp for rp in passes[done:] if rp[0] == final])
        finish(final, 0, 1)
        for r in range(final):
            finish(r, 3, 4)
        finish(final, 2, 4)
